import numpy as np
import ml_dtypes


def mxq(x, axis, fmt="e4m3"):
    dtype, down = {"e4m3": (ml_dtypes.float8_e4m3fn, 7), "e5m2": (ml_dtypes.float8_e5m2, 14)}[fmt]
    v = np.moveaxis(np.asarray(x, np.float32).astype(ml_dtypes.bfloat16).astype(np.float64), axis, -1)
    blocks = v.reshape(v.shape[:-1] + (-1, 32))
    amax = np.abs(blocks).max(-1, keepdims=True)
    byte = np.maximum(np.where(amax > 0, np.frexp(amax)[1] - 1 + 127, 0) - down, 1)
    scale = np.exp2(byte - 127.0)
    codes = (blocks / scale).astype(np.float32).astype(dtype).astype(np.float64)
    return np.moveaxis((codes * scale).reshape(v.shape), -1, axis)


WIDE = False


def mx_kscale(k):
    if not WIDE:
        return np.ones(k)
    levels = np.array([10, -10, 5, -5, 0])
    a = np.random.permutation(np.resize(levels, k // 512 * 4)).reshape(k // 512, 4)
    idx = np.arange(k)
    return np.exp2(a[idx // 512, idx % 128 // 32])


BF16 = ml_dtypes.bfloat16


def bf(x):
    return np.asarray(x, np.float32).astype(BF16)


def f64(x):
    return np.asarray(x).astype(np.float64)


E2M1 = np.array([0.0, 0.5, 1.0, 1.5, 2.0, 3.0, 4.0, 6.0, -0.0, -0.5, -1.0, -1.5, -2.0, -3.0, -4.0, -6.0])


def pack_weight(w, fmt):
    k, n = w.shape
    w = f64(bf(w)).reshape(k // 32, 32, n)
    amax = np.abs(w).max(1)
    if fmt == "e4m3":
        byte = np.frexp(amax)[1] - 1 + 127 - 7
    else:
        mant, ex = np.frexp(amax / 6.0)
        byte = np.where(mant > 0.5, ex, ex - 1) + 127
    byte = np.clip(np.where(amax > 0, byte, 1), 1, 254)
    scaled = (w * np.exp2(127.0 - byte)[:, None, :]).reshape(k, n).astype(np.float32)
    by_word = np.ascontiguousarray(scaled.reshape(k // 512, 128, 4, n).transpose(0, 1, 3, 2))
    if fmt == "e4m3":
        words = by_word.astype(ml_dtypes.float8_e4m3fn).view(np.uint8)
    else:
        c = by_word.astype(ml_dtypes.float4_e2m1fn).view(np.uint8) & 0xF
        words = c[..., 0::2] | (c[..., 1::2] << 4)
    return np.ascontiguousarray(words), np.ascontiguousarray(byte.astype(np.uint8).reshape(k // 512, 16, n))


def unpack_weight(words, scales, fmt):
    g, p, n, _ = words.shape
    if fmt == "e4m3":
        vals = np.ascontiguousarray(words).view(ml_dtypes.float8_e4m3fn).astype(np.float64)
    else:
        nib = np.empty((g, p, n, 4), np.uint8)
        nib[..., 0::2] = words & 0xF
        nib[..., 1::2] = words >> 4
        vals = E2M1[nib]
    vals = vals * np.repeat(np.exp2(scales.astype(np.float64) - 127.0), 8, axis=1)[..., None]
    return vals.transpose(0, 1, 3, 2).reshape(g * 512, n)

def pack4(w):
    words, scales = pack_weight(w, "e2m1")
    return words.reshape(words.shape[0], 128, -1), scales


def unpack4(words, scales):
    return unpack_weight(words.reshape(words.shape[0], 128, -1, 2), scales, "e2m1")


B, C, H, W = 2, 512, 64, 64
C2 = C + C


def setup_inputs():
    s = mx_kscale(C)
    x = bf(np.random.standard_normal((B, C, H, W)) * s[None, :, None, None])
    mask = bf(np.random.random_sample((B, 1, H, W)))
    words, scales = pack4(np.random.standard_normal((C, C2)) / np.sqrt(C) / s[:, None])
    b_kv = bf(np.random.standard_normal(C2) * 0.3)
    return {"x": x,
            "mask": mask,
            "W_kv_words": words,
            "W_kv_scales": scales,
            "b_kv": b_kv}


def reference(x, mask, W_kv_words, W_kv_scales, b_kv):
    x, mask = f64(x), f64(mask)
    b, c, h, w = x.shape
    xf = np.transpose(x, (0, 2, 3, 1)).reshape(b, h * w, c)
    kv = (mxq(xf, 2, "e4m3") @ unpack4(W_kv_words, W_kv_scales)) + f64(b_kv)
    k, v = kv[..., :c], kv[..., c:]
    k = k / np.linalg.norm(k, axis=-1, keepdims=True)
    m = np.transpose(mask, (0, 2, 3, 1)).reshape(b, h * w, 1)
    inv = 1.0 - m
    ku = k * inv
    km = k * m
    kv_know = np.sum(ku * v, axis=-2, keepdims=True)
    kv_mask = np.sum(km * v, axis=-2, keepdims=True)
    return kv_know, kv_mask

@@ -1,0 +1,239 @@
+import concourse.mybir as mybir
+from concourse.masks import make_identity
+
+FLOPS = 2 * 2 * 4096 * 512 * 1024
+
+F32 = mybir.dt.float32
+BF16 = mybir.dt.bfloat16
+U8 = mybir.dt.uint8
+U32 = mybir.dt.uint32
+I32 = mybir.dt.int32
+FP8X4 = mybir.dt.float8_e4m3fn_x4
+FP4X4 = mybir.dt.float4_e2m1fn_x4
+ALU = mybir.AluOpType
+ACT = mybir.ActivationFunctionType
+
+P = 128
+PACK = 4
+IMAGES = 2
+PIXELS = 4096
+CHANNELS = 512
+CHUNKS = CHANNELS // P
+TILE = 512
+STEPS = PIXELS // TILE
+LOAD = 1024
+
+
+STEPS_ALL = IMAGES * STEPS
+
+
+def tile_hydraattention_pa_t_kernel(tc, x, mask, w_words, w_scales, b_kv, out_know, out_mask):
+    nc = tc.nc
+    with tc.tile_pool(name="keep", bufs=1) as keep, tc.tile_pool(name="work", bufs=2) as work, tc.psum_pool(
+        name="psum", bufs=1
+    ) as psum, tc.manual_schedule():
+        w_plane = keep.tile([P, 2 * CHANNELS], U8, align_bytes=64)
+        nc.vector.memset(w_plane[:].bitcast(I32), 0)
+        for quad in range(4):
+            nc.sync.dma_start(
+                out=w_plane[32 * quad : 32 * quad + 4, :].bitcast(I32),
+                in_=w_scales[0, 4 * quad : 4 * quad + 4, :].bitcast(I32),
+            )
+        w_codes = keep.tile([P, 2 * 2 * CHANNELS], U8, align_bytes=64)
+        nc.sync.dma_start(out=w_codes[:].bitcast(I32), in_=w_words[0].bitcast(I32))
+
+        m_bc = keep.tile([P, IMAGES, PIXELS], BF16)
+        bias_rows = keep.tile([P, P], BF16)
+        nc.vector.memset(bias_rows[:], 0.0)
+        raw_tiles = []
+        for b in range(IMAGES):
+            x_rows = x[b].rearrange("(p j) h w -> p j (h w)", j=PACK)
+            for part in range(PIXELS // LOAD):
+                raw = keep.tile([P, PACK, LOAD], BF16, name="raw%d" % len(raw_tiles))
+                nc.sync.dma_start(out=raw[:], in_=x_rows[:, :, part * LOAD : (part + 1) * LOAD])
+                raw_tiles.append(raw)
+                if b == 0 and part == 0:
+                    nc.sync.dma_start(out=bias_rows[0:8, :], in_=b_kv.rearrange("(r c) -> r c", c=P))
+                if part == 1:
+                    nc.sync.dma_start(
+                        out=m_bc[:, b, :], in_=mask[b, 0].rearrange("h w -> (h w)").partition_broadcast(P)
+                    )
+
+        ident_bf = keep.tile([P, P], BF16)
+        make_identity(nc, ident_bf[:])
+        ident_f32 = keep.tile([P, P], F32)
+        make_identity(nc, ident_f32[:])
+        ones = keep.tile([P, P], F32)
+        nc.vector.memset(ones[:], 1.0)
+        result = keep.tile([P, P], F32)
+        nc.vector.memset(result[:], 0.0)
+
+        bias_ps = psum.tile([P, P], BF16, name="bias_ps", tag="norm")
+        nc.tensor.transpose(bias_ps[:], bias_rows[:], ident_bf[:])
+        bias = keep.tile([P, 2 * CHUNKS], F32)
+        nc.vector.tensor_copy(out=bias[:], in_=bias_ps[:, 0 : 2 * CHUNKS])
+
+        sums_all = keep.tile([P, IMAGES * CHUNKS, STEPS], F32)
+        sums_mask = keep.tile([P, IMAGES * CHUNKS, STEPS], F32)
+
+        grouped_of = {}
+        codes_of = {}
+        keys_of = {}
+        inv_norm_of = {}
+        khats_of = {}
+        values_of = {}
+
+        def regroup(s):
+            if s >= STEPS_ALL:
+                return
+            raw = raw_tiles[s * TILE // LOAD]
+            first = s * TILE % LOAD
+            grouped = work.tile([P, TILE, PACK], BF16, name="grouped", tag="grouped", bufs=3, align_bytes=64)
+            nc.scalar.copy(
+                out=grouped[:].rearrange("p (c i) j -> p c j i", i=4),
+                in_=raw[:, :, first : first + TILE].rearrange("p j (c i) -> p c j i", i=4),
+            )
+            grouped_of[s] = grouped
+
+        def quantise(s):
+            if s >= STEPS_ALL:
+                return
+            x_codes = work.tile([P, TILE], U32, name="x_codes", tag="x_codes", bufs=4, align_bytes=64)
+            x_plane = work.tile([P, TILE], U8, name="x_plane", tag="x_plane", bufs=4, align_bytes=64)
+            nc.vector.quantize_mx(
+                out=x_codes[:].bitcast(FP8X4),
+                scales=x_plane[:],
+                in_=grouped_of[s][:].rearrange("p t j -> p (t j)"),
+            )
+            codes_of[s] = (x_codes, x_plane)
+
+        def project(acc, s, chunk):
+            x_codes, x_plane = codes_of[s]
+            nc.tensor.matmul_mx(
+                out=acc[:],
+                lhsT=w_codes[:, 2 * P * chunk : 2 * P * (chunk + 1)].bitcast(FP4X4),
+                lhsT_scale=w_plane[:, P * chunk : P * (chunk + 1)],
+                rhs=x_codes[:].bitcast(FP8X4),
+                rhs_scale=x_plane[:],
+                start=True,
+                stop=True,
+            )
+
+        def value_pass(s, chunk):
+            if s >= STEPS_ALL:
+                return
+            value = psum.tile([P, TILE], F32, name="value", tag="value", bufs=3)
+            project(value, s, CHUNKS + chunk)
+            values_of[(s, chunk)] = value
+
+        def keys_and_squares(s):
+            keys = []
+            squares = []
+            for chunk in range(CHUNKS):
+                key = psum.tile([P, TILE], F32, name="key", tag="key", bufs=CHUNKS)
+                project(key, s, chunk)
+                keys.append(key)
+                square = work.tile([P, TILE], F32, name="square", tag="square", bufs=6)
+                nc.scalar.activation(
+                    out=square[:], in_=key[:], func=ACT.Square, bias=bias[:, chunk : chunk + 1], scale=1.0
+                )
+                squares.append(square)
+            keys_of[s] = keys
+            pair = work.tile([P, TILE], F32, name="pair", tag="pair", bufs=2)
+            nc.gpsimd.tensor_tensor(out=pair[:], in0=squares[0][:], in1=squares[1][:], op=ALU.add)
+            return [squares[2], squares[3], pair]
+
+        def khat_pass(s, chunk):
+            khat = work.tile([P, TILE], F32, name="khat", tag="khat", bufs=CHUNKS)
+            nc.vector.scalar_tensor_tensor(
+                out=khat[:],
+                in0=keys_of[s][chunk][:],
+                scalar=bias[:, chunk : chunk + 1],
+                in1=inv_norm_of[s][:],
+                op0=ALU.add,
+                op1=ALU.mult,
+            )
+            khats_of[(s, chunk)] = khat
+
+        def pool_pixels(s, chunk):
+            b = s // STEPS
+            step = s % STEPS
+            column = b * CHUNKS + chunk
+            product = work.tile([P, TILE], F32, name="product", tag="product", bufs=3)
+            nc.vector.scalar_tensor_tensor(
+                out=product[:],
+                in0=values_of[(s, chunk)][:],
+                scalar=bias[:, CHUNKS + chunk : CHUNKS + chunk + 1],
+                in1=khats_of[(s, chunk)][:],
+                op0=ALU.add,
+                op1=ALU.mult,
+                accum_out=sums_all[:, column, step : step + 1],
+            )
+            weighted = work.tile([P, TILE], F32, name="weighted", tag="weighted", bufs=2)
+            nc.vector.scalar_tensor_tensor(
+                out=weighted[:],
+                in0=product[:],
+                scalar=1.0,
+                in1=m_bc[:, b, step * TILE : (step + 1) * TILE],
+                op0=ALU.mult,
+                op1=ALU.mult,
+                accum_out=sums_mask[:, column, step : step + 1],
+            )
+
+        def norm_pass(norm, addend, first, last):
+            nc.tensor.matmul(out=norm[:], lhsT=ones[:], rhs=addend[:], start=first, stop=last)
+
+        def invert_norm(s, norm):
+            inv_norm = work.tile([P, TILE], F32, name="inv_norm", tag="inv_norm", bufs=2)
+            nc.scalar.activation(out=inv_norm[:], in_=norm[:], func=ACT.Abs_reciprocal_sqrt)
+            inv_norm_of[s] = inv_norm
+
+        regroup(0)
+        regroup(1)
+        quantise(0)
+        regroup(2)
+        quantise(1)
+        addends = keys_and_squares(0)
+        norm = psum.tile([P, TILE], F32, name="norm", tag="norm")
+        norm_pass(norm, addends[0], True, False)
+        norm_pass(norm, addends[1], False, False)
+        norm_pass(norm, addends[2], False, True)
+        invert_norm(0, norm)
+        for chunk in range(CHUNKS - 1):
+            value_pass(0, chunk)
+
+        for s in range(STEPS_ALL):
+            follows = s + 1 < STEPS_ALL
+            for chunk in range(CHUNKS):
+                khat_pass(s, chunk)
+            quantise(s + 2)
+            if follows:
+                addends = keys_and_squares(s + 1)
+                regroup(s + 3)
+                norm = psum.tile([P, TILE], F32, name="norm", tag="norm")
+                norm_pass(norm, addends[0], True, False)
+            pool_pixels(s, 0)
+            value_pass(s, CHUNKS - 1)
+            if follows:
+                norm_pass(norm, addends[1], False, False)
+                norm_pass(norm, addends[2], False, True)
+                invert_norm(s + 1, norm)
+            for chunk in range(1, CHUNKS):
+                pool_pixels(s, chunk)
+                value_pass(s + 1, chunk - 1)
+
+        groups = IMAGES * CHUNKS
+        total = keep.tile([P, groups], F32)
+        nc.vector.tensor_reduce(out=total[:], in_=sums_all[:], axis=mybir.AxisListType.X, op=ALU.add)
+        nc.vector.tensor_reduce(
+            out=result[:, groups : 2 * groups], in_=sums_mask[:], axis=mybir.AxisListType.X, op=ALU.add
+        )
+        nc.vector.tensor_tensor(
+            out=result[:, 0:groups], in0=total[:], in1=result[:, groups : 2 * groups], op=ALU.subtract
+        )
+        rows_ps = psum.tile([P, P], F32, name="rows_ps", tag="norm")
+        nc.tensor.transpose(rows_ps[:], result[:], ident_f32[:])
+        rows = keep.tile([2 * groups, P], F32)
+        nc.scalar.copy(out=rows[:], in_=rows_ps[0 : 2 * groups, :])
+        nc.sync.dma_start(out=out_know.rearrange("b o (j p) -> (b o j) p", p=P), in_=rows[0:groups, :])
+        nc.sync.dma_start(out=out_mask.rearrange("b o (j p) -> (b o j) p", p=P), in_=rows[groups : 2 * groups, :])

@@ -25,6 +25,7 @@ LOAD = 1024
 
 
 STEPS_ALL = IMAGES * STEPS
+AHEAD = 5
 
 
 def tile_hydraattention_pa_t_kernel(tc, x, mask, w_words, w_scales, b_kv, out_know, out_mask):
@@ -45,6 +46,7 @@ def tile_hydraattention_pa_t_kernel(tc, x, mask, w_words, w_scales, b_kv, out_kn
         m_bc = keep.tile([P, IMAGES, PIXELS], BF16)
         bias_rows = keep.tile([P, P], BF16)
         nc.vector.memset(bias_rows[:], 0.0)
+        nc.sync.dma_start(out=bias_rows[0 : 2 * CHUNKS, :], in_=b_kv.rearrange("(r c) -> r c", c=P))
         raw_tiles = []
         for b in range(IMAGES):
             x_rows = x[b].rearrange("(p j) h w -> p j (h w)", j=PACK)
@@ -52,8 +54,6 @@ def tile_hydraattention_pa_t_kernel(tc, x, mask, w_words, w_scales, b_kv, out_kn
                 raw = keep.tile([P, PACK, LOAD], BF16, name="raw%d" % len(raw_tiles))
                 nc.sync.dma_start(out=raw[:], in_=x_rows[:, :, part * LOAD : (part + 1) * LOAD])
                 raw_tiles.append(raw)
-                if b == 0 and part == 0:
-                    nc.sync.dma_start(out=bias_rows[0:8, :], in_=b_kv.rearrange("(r c) -> r c", c=P))
                 if part == 1:
                     nc.sync.dma_start(
                         out=m_bc[:, b, :], in_=mask[b, 0].rearrange("h w -> (h w)").partition_broadcast(P)
@@ -78,18 +78,19 @@ def tile_hydraattention_pa_t_kernel(tc, x, mask, w_words, w_scales, b_kv, out_kn
 
         grouped_of = {}
         codes_of = {}
-        keys_of = {}
+        pairs_of = {}
+        norm_of = {}
         inv_norm_of = {}
+        banks = {}
         khats_of = {}
-        values_of = {}
 
-        def regroup(s):
+        def regroup(s, copy):
             if s >= STEPS_ALL:
                 return
             raw = raw_tiles[s * TILE // LOAD]
             first = s * TILE % LOAD
             grouped = work.tile([P, TILE, PACK], BF16, name="grouped", tag="grouped", bufs=3, align_bytes=64)
-            nc.scalar.copy(
+            copy(
                 out=grouped[:].rearrange("p (c i) j -> p c j i", i=4),
                 in_=raw[:, :, first : first + TILE].rearrange("p j (c i) -> p c j i", i=4),
             )
@@ -98,8 +99,8 @@ def tile_hydraattention_pa_t_kernel(tc, x, mask, w_words, w_scales, b_kv, out_kn
         def quantise(s):
             if s >= STEPS_ALL:
                 return
-            x_codes = work.tile([P, TILE], U32, name="x_codes", tag="x_codes", bufs=4, align_bytes=64)
-            x_plane = work.tile([P, TILE], U8, name="x_plane", tag="x_plane", bufs=4, align_bytes=64)
+            x_codes = work.tile([P, TILE], U32, name="x_codes", tag="x_codes", bufs=5, align_bytes=64)
+            x_plane = work.tile([P, TILE], U8, name="x_plane", tag="x_plane", bufs=5, align_bytes=64)
             nc.vector.quantize_mx(
                 out=x_codes[:].bitcast(FP8X4),
                 scales=x_plane[:],
@@ -107,53 +108,70 @@ def tile_hydraattention_pa_t_kernel(tc, x, mask, w_words, w_scales, b_kv, out_kn
             )
             codes_of[s] = (x_codes, x_plane)
 
-        def project(acc, s, chunk):
+        def project(acc, s, column_chunk):
             x_codes, x_plane = codes_of[s]
             nc.tensor.matmul_mx(
                 out=acc[:],
-                lhsT=w_codes[:, 2 * P * chunk : 2 * P * (chunk + 1)].bitcast(FP4X4),
-                lhsT_scale=w_plane[:, P * chunk : P * (chunk + 1)],
+                lhsT=w_codes[:, 2 * P * column_chunk : 2 * P * (column_chunk + 1)].bitcast(FP4X4),
+                lhsT_scale=w_plane[:, P * column_chunk : P * (column_chunk + 1)],
                 rhs=x_codes[:].bitcast(FP8X4),
                 rhs_scale=x_plane[:],
                 start=True,
                 stop=True,
             )
 
-        def value_pass(s, chunk):
+        def square_key(s, chunk):
             if s >= STEPS_ALL:
                 return
-            value = psum.tile([P, TILE], F32, name="value", tag="value", bufs=3)
-            project(value, s, CHUNKS + chunk)
-            values_of[(s, chunk)] = value
+            key = psum.tile([P, TILE], F32, name="key", tag="key", bufs=2)
+            project(key, s, chunk)
+            square = work.tile([P, TILE], F32, name="square", tag="square", bufs=4)
+            nc.scalar.activation(
+                out=square[:], in_=key[:], func=ACT.Square, bias=bias[:, chunk : chunk + 1], scale=1.0
+            )
+            if chunk % 2 == 0:
+                pairs_of[s] = pairs_of.get(s, []) + [square]
+            else:
+                pair = work.tile([P, TILE], F32, name="pair", tag="pair", bufs=6)
+                nc.gpsimd.tensor_tensor(out=pair[:], in0=pairs_of[s][-1][:], in1=square[:], op=ALU.add)
+                pairs_of[s][-1] = pair
 
-        def keys_and_squares(s):
-            keys = []
-            squares = []
-            for chunk in range(CHUNKS):
-                key = psum.tile([P, TILE], F32, name="key", tag="key", bufs=CHUNKS)
-                project(key, s, chunk)
-                keys.append(key)
-                square = work.tile([P, TILE], F32, name="square", tag="square", bufs=6)
-                nc.scalar.activation(
-                    out=square[:], in_=key[:], func=ACT.Square, bias=bias[:, chunk : chunk + 1], scale=1.0
-                )
-                squares.append(square)
-            keys_of[s] = keys
-            pair = work.tile([P, TILE], F32, name="pair", tag="pair", bufs=2)
-            nc.gpsimd.tensor_tensor(out=pair[:], in0=squares[0][:], in1=squares[1][:], op=ALU.add)
-            return [squares[2], squares[3], pair]
+        def norm_pass(s, half):
+            if s >= STEPS_ALL:
+                return
+            if half == 0:
+                norm_of[s] = psum.tile([P, TILE], F32, name="norm", tag="norm")
+            nc.tensor.matmul(
+                out=norm_of[s][:], lhsT=ones[:], rhs=pairs_of[s][half][:], start=(half == 0), stop=(half == 1)
+            )
+
+        def invert_norm(s):
+            if s >= STEPS_ALL:
+                return
+            inv_norm = work.tile([P, TILE], F32, name="inv_norm", tag="inv_norm", bufs=2)
+            nc.scalar.activation(out=inv_norm[:], in_=norm_of[s][:], func=ACT.Abs_reciprocal_sqrt)
+            inv_norm_of[s] = inv_norm
+
+        def feed(n):
+            s = n // (2 * CHUNKS)
+            if s >= STEPS_ALL:
+                return
+            bank = psum.tile([P, TILE], F32, name="bank", tag="bank", bufs=AHEAD)
+            project(bank, s, n % (2 * CHUNKS))
+            banks[n] = bank
 
         def khat_pass(s, chunk):
             khat = work.tile([P, TILE], F32, name="khat", tag="khat", bufs=CHUNKS)
             nc.vector.scalar_tensor_tensor(
                 out=khat[:],
-                in0=keys_of[s][chunk][:],
+                in0=banks[2 * CHUNKS * s + chunk][:],
                 scalar=bias[:, chunk : chunk + 1],
                 in1=inv_norm_of[s][:],
                 op0=ALU.add,
                 op1=ALU.mult,
             )
             khats_of[(s, chunk)] = khat
+            feed(2 * CHUNKS * s + chunk + AHEAD)
 
         def pool_pixels(s, chunk):
             b = s // STEPS
@@ -162,13 +180,14 @@ def tile_hydraattention_pa_t_kernel(tc, x, mask, w_words, w_scales, b_kv, out_kn
             product = work.tile([P, TILE], F32, name="product", tag="product", bufs=3)
             nc.vector.scalar_tensor_tensor(
                 out=product[:],
-                in0=values_of[(s, chunk)][:],
+                in0=banks[2 * CHUNKS * s + CHUNKS + chunk][:],
                 scalar=bias[:, CHUNKS + chunk : CHUNKS + chunk + 1],
                 in1=khats_of[(s, chunk)][:],
                 op0=ALU.add,
                 op1=ALU.mult,
                 accum_out=sums_all[:, column, step : step + 1],
             )
+            feed(2 * CHUNKS * s + CHUNKS + chunk + AHEAD)
             weighted = work.tile([P, TILE], F32, name="weighted", tag="weighted", bufs=2)
             nc.vector.scalar_tensor_tensor(
                 out=weighted[:],
@@ -180,47 +199,32 @@ def tile_hydraattention_pa_t_kernel(tc, x, mask, w_words, w_scales, b_kv, out_kn
                 accum_out=sums_mask[:, column, step : step + 1],
             )
 
-        def norm_pass(norm, addend, first, last):
-            nc.tensor.matmul(out=norm[:], lhsT=ones[:], rhs=addend[:], start=first, stop=last)
-
-        def invert_norm(s, norm):
-            inv_norm = work.tile([P, TILE], F32, name="inv_norm", tag="inv_norm", bufs=2)
-            nc.scalar.activation(out=inv_norm[:], in_=norm[:], func=ACT.Abs_reciprocal_sqrt)
-            inv_norm_of[s] = inv_norm
-
-        regroup(0)
-        regroup(1)
-        quantise(0)
-        regroup(2)
-        quantise(1)
-        addends = keys_and_squares(0)
-        norm = psum.tile([P, TILE], F32, name="norm", tag="norm")
-        norm_pass(norm, addends[0], True, False)
-        norm_pass(norm, addends[1], False, False)
-        norm_pass(norm, addends[2], False, True)
-        invert_norm(0, norm)
-        for chunk in range(CHUNKS - 1):
-            value_pass(0, chunk)
+        for s in range(4):
+            regroup(s, nc.vector.tensor_copy)
+            if s < 3:
+                quantise(s)
+        for chunk in range(CHUNKS):
+            square_key(0, chunk)
+        norm_pass(0, 0)
+        norm_pass(0, 1)
+        invert_norm(0)
+        for chunk in range(CHUNKS):
+            square_key(1, chunk)
+        for n in range(AHEAD):
+            feed(n)
 
         for s in range(STEPS_ALL):
-            follows = s + 1 < STEPS_ALL
+            regroup(s + 4, nc.scalar.copy)
             for chunk in range(CHUNKS):
                 khat_pass(s, chunk)
-            quantise(s + 2)
-            if follows:
-                addends = keys_and_squares(s + 1)
-                regroup(s + 3)
-                norm = psum.tile([P, TILE], F32, name="norm", tag="norm")
-                norm_pass(norm, addends[0], True, False)
-            pool_pixels(s, 0)
-            value_pass(s, CHUNKS - 1)
-            if follows:
-                norm_pass(norm, addends[1], False, False)
-                norm_pass(norm, addends[2], False, True)
-                invert_norm(s + 1, norm)
-            for chunk in range(1, CHUNKS):
+                if chunk < 2:
+                    norm_pass(s + 1, chunk)
+                if chunk == 1:
+                    invert_norm(s + 1)
+            quantise(s + 3)
+            for chunk in range(CHUNKS):
                 pool_pixels(s, chunk)
-                value_pass(s + 1, chunk - 1)
+                square_key(s + 2, chunk)
 
         groups = IMAGES * CHUNKS
         total = keep.tile([P, groups], F32)

@@ -25,7 +25,7 @@ LOAD = 1024
 
 
 STEPS_ALL = IMAGES * STEPS
-AHEAD = 5
+AHEAD = 4
 
 
 def tile_hydraattention_pa_t_kernel(tc, x, mask, w_words, w_scales, b_kv, out_know, out_mask):
@@ -43,7 +43,8 @@ def tile_hydraattention_pa_t_kernel(tc, x, mask, w_words, w_scales, b_kv, out_kn
         w_codes = keep.tile([P, 2 * 2 * CHANNELS], U8, align_bytes=64)
         nc.sync.dma_start(out=w_codes[:].bitcast(I32), in_=w_words[0].bitcast(I32))
 
-        m_bc = keep.tile([P, IMAGES, PIXELS], BF16)
+        mask_rows = keep.tile([P, IMAGES * PIXELS], BF16)
+        nc.vector.memset(mask_rows[:].bitcast(I32), 0)
         bias_rows = keep.tile([P, P], BF16)
         nc.vector.memset(bias_rows[:], 0.0)
         nc.sync.dma_start(out=bias_rows[0 : 2 * CHUNKS, :], in_=b_kv.rearrange("(r c) -> r c", c=P))
@@ -54,10 +55,8 @@ def tile_hydraattention_pa_t_kernel(tc, x, mask, w_words, w_scales, b_kv, out_kn
                 raw = keep.tile([P, PACK, LOAD], BF16, name="raw%d" % len(raw_tiles))
                 nc.sync.dma_start(out=raw[:], in_=x_rows[:, :, part * LOAD : (part + 1) * LOAD])
                 raw_tiles.append(raw)
-                if part == 1:
-                    nc.sync.dma_start(
-                        out=m_bc[:, b, :], in_=mask[b, 0].rearrange("h w -> (h w)").partition_broadcast(P)
-                    )
+                if b == 0 and part == 0:
+                    nc.sync.dma_start(out=mask_rows[0:1, :], in_=mask.rearrange("b o h w -> (b o h w)").unsqueeze(0))
 
         ident_bf = keep.tile([P, P], BF16)
         make_identity(nc, ident_bf[:])
@@ -65,6 +64,8 @@ def tile_hydraattention_pa_t_kernel(tc, x, mask, w_words, w_scales, b_kv, out_kn
         make_identity(nc, ident_f32[:])
         ones = keep.tile([P, P], F32)
         nc.vector.memset(ones[:], 1.0)
+        ones_bf = keep.tile([P, P], BF16)
+        nc.vector.memset(ones_bf[:], 1.0)
         result = keep.tile([P, P], F32)
         nc.vector.memset(result[:], 0.0)
 
@@ -82,6 +83,7 @@ def tile_hydraattention_pa_t_kernel(tc, x, mask, w_words, w_scales, b_kv, out_kn
         norm_of = {}
         inv_norm_of = {}
         banks = {}
+        mask_of = {}
         khats_of = {}
 
         def regroup(s, copy):
@@ -152,6 +154,15 @@ def tile_hydraattention_pa_t_kernel(tc, x, mask, w_words, w_scales, b_kv, out_kn
             nc.scalar.activation(out=inv_norm[:], in_=norm_of[s][:], func=ACT.Abs_reciprocal_sqrt)
             inv_norm_of[s] = inv_norm
 
+        def spread_mask(s):
+            if s >= STEPS_ALL:
+                return
+            mask_ps = psum.tile([P, TILE], F32, name="mask_ps", tag="mask_ps")
+            nc.tensor.matmul(
+                out=mask_ps[:], lhsT=ones_bf[:], rhs=mask_rows[:, s * TILE : (s + 1) * TILE], start=True, stop=True
+            )
+            mask_of[s] = mask_ps
+
         def feed(n):
             s = n // (2 * CHUNKS)
             if s >= STEPS_ALL:
@@ -191,9 +202,9 @@ def tile_hydraattention_pa_t_kernel(tc, x, mask, w_words, w_scales, b_kv, out_kn
             weighted = work.tile([P, TILE], F32, name="weighted", tag="weighted", bufs=2)
             nc.vector.scalar_tensor_tensor(
                 out=weighted[:],
-                in0=product[:],
+                in0=mask_of[s][:],
                 scalar=1.0,
-                in1=m_bc[:, b, step * TILE : (step + 1) * TILE],
+                in1=product[:],
                 op0=ALU.mult,
                 op1=ALU.mult,
                 accum_out=sums_mask[:, column, step : step + 1],
@@ -210,6 +221,7 @@ def tile_hydraattention_pa_t_kernel(tc, x, mask, w_words, w_scales, b_kv, out_kn
         invert_norm(0)
         for chunk in range(CHUNKS):
             square_key(1, chunk)
+        spread_mask(0)
         for n in range(AHEAD):
             feed(n)
 
@@ -225,6 +237,7 @@ def tile_hydraattention_pa_t_kernel(tc, x, mask, w_words, w_scales, b_kv, out_kn
             for chunk in range(CHUNKS):
                 pool_pixels(s, chunk)
                 square_key(s + 2, chunk)
+            spread_mask(s + 1)
 
         groups = IMAGES * CHUNKS
         total = keep.tile([P, groups], F32)

@@ -21,7 +21,7 @@ CHANNELS = 512
 CHUNKS = CHANNELS // P
 TILE = 512
 STEPS = PIXELS // TILE
-LOAD = 1024
+VECTOR_CHUNKS = 2
 
 
 STEPS_ALL = IMAGES * STEPS
@@ -43,20 +43,21 @@ def tile_hydraattention_pa_t_kernel(tc, x, mask, w_words, w_scales, b_kv, out_kn
         w_codes = keep.tile([P, 2 * 2 * CHANNELS], U8, align_bytes=64)
         nc.sync.dma_start(out=w_codes[:].bitcast(I32), in_=w_words[0].bitcast(I32))
 
-        mask_rows = keep.tile([P, IMAGES * PIXELS], BF16)
-        nc.vector.memset(mask_rows[:].bitcast(I32), 0)
+        m_bc = keep.tile([P, IMAGES, PIXELS], BF16)
         bias_rows = keep.tile([P, P], BF16)
         nc.vector.memset(bias_rows[:], 0.0)
         nc.sync.dma_start(out=bias_rows[0 : 2 * CHUNKS, :], in_=b_kv.rearrange("(r c) -> r c", c=P))
         raw_tiles = []
         for b in range(IMAGES):
             x_rows = x[b].rearrange("(p j) h w -> p j (h w)", j=PACK)
-            for part in range(PIXELS // LOAD):
-                raw = keep.tile([P, PACK, LOAD], BF16, name="raw%d" % len(raw_tiles))
-                nc.sync.dma_start(out=raw[:], in_=x_rows[:, :, part * LOAD : (part + 1) * LOAD])
+            for step in range(STEPS):
+                raw = keep.tile([P, PACK, TILE], BF16, name="raw%d" % len(raw_tiles))
+                nc.sync.dma_start(out=raw[:], in_=x_rows[:, :, step * TILE : (step + 1) * TILE])
                 raw_tiles.append(raw)
-                if b == 0 and part == 0:
-                    nc.sync.dma_start(out=mask_rows[0:1, :], in_=mask.rearrange("b o h w -> (b o h w)").unsqueeze(0))
+                if step == 1:
+                    nc.sync.dma_start(
+                        out=m_bc[:, b, :], in_=mask[b, 0].rearrange("h w -> (h w)").partition_broadcast(P)
+                    )
 
         ident_bf = keep.tile([P, P], BF16)
         make_identity(nc, ident_bf[:])
@@ -64,8 +65,9 @@ def tile_hydraattention_pa_t_kernel(tc, x, mask, w_words, w_scales, b_kv, out_kn
         make_identity(nc, ident_f32[:])
         ones = keep.tile([P, P], F32)
         nc.vector.memset(ones[:], 1.0)
-        ones_bf = keep.tile([P, P], BF16)
-        nc.vector.memset(ones_bf[:], 1.0)
+        first_row = keep.tile([P, P], BF16)
+        nc.vector.memset(first_row[:], 0.0)
+        nc.vector.memset(first_row[0:1, :], 1.0)
         result = keep.tile([P, P], F32)
         nc.vector.memset(result[:], 0.0)
 
@@ -75,7 +77,8 @@ def tile_hydraattention_pa_t_kernel(tc, x, mask, w_words, w_scales, b_kv, out_kn
         nc.vector.tensor_copy(out=bias[:], in_=bias_ps[:, 0 : 2 * CHUNKS])
 
         sums_all = keep.tile([P, IMAGES * CHUNKS, STEPS], F32)
-        sums_mask = keep.tile([P, IMAGES * CHUNKS, STEPS], F32)
+        sums_mask_v = keep.tile([P, IMAGES, VECTOR_CHUNKS, STEPS], F32)
+        sums_mask_s = keep.tile([P, IMAGES, CHUNKS - VECTOR_CHUNKS, STEPS], F32)
 
         grouped_of = {}
         codes_of = {}
@@ -84,17 +87,16 @@ def tile_hydraattention_pa_t_kernel(tc, x, mask, w_words, w_scales, b_kv, out_kn
         inv_norm_of = {}
         banks = {}
         mask_of = {}
+        weighted_of = {}
         khats_of = {}
 
         def regroup(s, copy):
             if s >= STEPS_ALL:
                 return
-            raw = raw_tiles[s * TILE // LOAD]
-            first = s * TILE % LOAD
             grouped = work.tile([P, TILE, PACK], BF16, name="grouped", tag="grouped", bufs=3, align_bytes=64)
             copy(
                 out=grouped[:].rearrange("p (c i) j -> p c j i", i=4),
-                in_=raw[:, :, first : first + TILE].rearrange("p j (c i) -> p c j i", i=4),
+                in_=raw_tiles[s][:].rearrange("p j (c i) -> p c j i", i=4),
             )
             grouped_of[s] = grouped
 
@@ -159,7 +161,11 @@ def tile_hydraattention_pa_t_kernel(tc, x, mask, w_words, w_scales, b_kv, out_kn
                 return
             mask_ps = psum.tile([P, TILE], F32, name="mask_ps", tag="mask_ps")
             nc.tensor.matmul(
-                out=mask_ps[:], lhsT=ones_bf[:], rhs=mask_rows[:, s * TILE : (s + 1) * TILE], start=True, stop=True
+                out=mask_ps[:],
+                lhsT=first_row[:],
+                rhs=m_bc[:, s // STEPS, s % STEPS * TILE : (s % STEPS + 1) * TILE],
+                start=True,
+                stop=True,
             )
             mask_of[s] = mask_ps
 
@@ -188,7 +194,7 @@ def tile_hydraattention_pa_t_kernel(tc, x, mask, w_words, w_scales, b_kv, out_kn
             b = s // STEPS
             step = s % STEPS
             column = b * CHUNKS + chunk
-            product = work.tile([P, TILE], F32, name="product", tag="product", bufs=3)
+            product = work.tile([P, TILE], F32, name="product", tag="product", bufs=5)
             nc.vector.scalar_tensor_tensor(
                 out=product[:],
                 in0=banks[2 * CHUNKS * s + CHUNKS + chunk][:],
@@ -199,16 +205,35 @@ def tile_hydraattention_pa_t_kernel(tc, x, mask, w_words, w_scales, b_kv, out_kn
                 accum_out=sums_all[:, column, step : step + 1],
             )
             feed(2 * CHUNKS * s + CHUNKS + chunk + AHEAD)
-            weighted = work.tile([P, TILE], F32, name="weighted", tag="weighted", bufs=2)
-            nc.vector.scalar_tensor_tensor(
-                out=weighted[:],
-                in0=mask_of[s][:],
-                scalar=1.0,
-                in1=product[:],
-                op0=ALU.mult,
-                op1=ALU.mult,
-                accum_out=sums_mask[:, column, step : step + 1],
-            )
+            if chunk < VECTOR_CHUNKS:
+                unused = work.tile([P, TILE], F32, name="unused", tag="unused", bufs=2)
+                nc.vector.scalar_tensor_tensor(
+                    out=unused[:],
+                    in0=mask_of[s][:],
+                    scalar=1.0,
+                    in1=product[:],
+                    op0=ALU.mult,
+                    op1=ALU.mult,
+                    accum_out=sums_mask_v[:, b, chunk, step : step + 1],
+                )
+            else:
+                weighted = work.tile([P, TILE], F32, name="weighted", tag="weighted", bufs=6)
+                nc.gpsimd.tensor_tensor(
+                    out=weighted[:], in0=product[:], in1=m_bc[:, b, step * TILE : (step + 1) * TILE], op=ALU.mult
+                )
+                weighted_of[(s, chunk)] = weighted
+
+        def sum_weighted(s):
+            if s < 0:
+                return
+            for chunk in range(VECTOR_CHUNKS, CHUNKS):
+                unread = work.tile([P, TILE], BF16, name="unread", tag="unread", bufs=2)
+                nc.scalar.activation(
+                    out=unread[:],
+                    in_=weighted_of[(s, chunk)][:],
+                    func=ACT.Copy,
+                    accum_out=sums_mask_s[:, s // STEPS, chunk - VECTOR_CHUNKS, s % STEPS : s % STEPS + 1],
+                )
 
         for s in range(4):
             regroup(s, nc.vector.tensor_copy)
@@ -226,6 +251,7 @@ def tile_hydraattention_pa_t_kernel(tc, x, mask, w_words, w_scales, b_kv, out_kn
             feed(n)
 
         for s in range(STEPS_ALL):
+            sum_weighted(s - 1)
             regroup(s + 4, nc.scalar.copy)
             for chunk in range(CHUNKS):
                 khat_pass(s, chunk)
@@ -239,11 +265,16 @@ def tile_hydraattention_pa_t_kernel(tc, x, mask, w_words, w_scales, b_kv, out_kn
                 square_key(s + 2, chunk)
             spread_mask(s + 1)
 
+        sum_weighted(STEPS_ALL - 1)
         groups = IMAGES * CHUNKS
         total = keep.tile([P, groups], F32)
         nc.vector.tensor_reduce(out=total[:], in_=sums_all[:], axis=mybir.AxisListType.X, op=ALU.add)
+        masked = result[:, groups : 2 * groups].rearrange("p (b c) -> p b c", b=IMAGES)
         nc.vector.tensor_reduce(
-            out=result[:, groups : 2 * groups], in_=sums_mask[:], axis=mybir.AxisListType.X, op=ALU.add
+            out=masked[:, :, 0:VECTOR_CHUNKS], in_=sums_mask_v[:], axis=mybir.AxisListType.X, op=ALU.add
+        )
+        nc.vector.tensor_reduce(
+            out=masked[:, :, VECTOR_CHUNKS:CHUNKS], in_=sums_mask_s[:], axis=mybir.AxisListType.X, op=ALU.add
         )
         nc.vector.tensor_tensor(
             out=result[:, 0:groups], in0=total[:], in1=result[:, groups : 2 * groups], op=ALU.subtract

@@ -152,7 +152,7 @@ def tile_hydraattention_pa_t_kernel(tc, x, mask, w_words, w_scales, b_kv, out_kn
         def invert_norm(s):
             if s >= STEPS_ALL:
                 return
-            inv_norm = work.tile([P, TILE], F32, name="inv_norm", tag="inv_norm", bufs=2)
+            inv_norm = work.tile([P, TILE], F32, name="inv_norm", tag="inv_norm", bufs=3)
             nc.scalar.activation(out=inv_norm[:], in_=norm_of[s][:], func=ACT.Abs_reciprocal_sqrt)
             inv_norm_of[s] = inv_norm
 
@@ -246,23 +246,26 @@ def tile_hydraattention_pa_t_kernel(tc, x, mask, w_words, w_scales, b_kv, out_kn
         invert_norm(0)
         for chunk in range(CHUNKS):
             square_key(1, chunk)
+        norm_pass(1, 0)
+        norm_pass(1, 1)
+        invert_norm(1)
         spread_mask(0)
         for n in range(AHEAD):
             feed(n)
 
         for s in range(STEPS_ALL):
-            sum_weighted(s - 1)
-            regroup(s + 4, nc.scalar.copy)
             for chunk in range(CHUNKS):
                 khat_pass(s, chunk)
-                if chunk < 2:
-                    norm_pass(s + 1, chunk)
-                if chunk == 1:
-                    invert_norm(s + 1)
+                square_key(s + 2, chunk)
             quantise(s + 3)
+            regroup(s + 4, nc.scalar.copy)
+            sum_weighted(s - 1)
             for chunk in range(CHUNKS):
                 pool_pixels(s, chunk)
-                square_key(s + 2, chunk)
+                if chunk < 2:
+                    norm_pass(s + 2, chunk)
+                if chunk == 1:
+                    invert_norm(s + 2)
             spread_mask(s + 1)
 
         sum_weighted(STEPS_ALL - 1)

@@ -21,11 +21,16 @@ CHANNELS = 512
 CHUNKS = CHANNELS // P
 TILE = 512
 STEPS = PIXELS // TILE
-VECTOR_CHUNKS = 2
-
-
 STEPS_ALL = IMAGES * STEPS
-AHEAD = 4
+HALVES = 2
+GPSIMD_CHUNKS = 2
+
+KEY_BANKS = 2
+AHEAD = 8 - KEY_BANKS - 2
+
+NORM_AHEAD = 2
+QUANTISE_AHEAD = 3
+REGROUP_AHEAD = 4
 
 
 def tile_hydraattention_pa_t_kernel(tc, x, mask, w_words, w_scales, b_kv, out_know, out_mask):
@@ -33,6 +38,16 @@ def tile_hydraattention_pa_t_kernel(tc, x, mask, w_words, w_scales, b_kv, out_kn
     with tc.tile_pool(name="keep", bufs=1) as keep, tc.tile_pool(name="work", bufs=2) as work, tc.psum_pool(
         name="psum", bufs=1
     ) as psum, tc.manual_schedule():
+        raw_tiles = []
+
+        def load_step(s):
+            x_rows = x[s // STEPS].rearrange("(p j) h w -> p j (h w)", j=PACK)
+            raw = keep.tile([P, PACK, TILE], BF16, name="raw%d" % s)
+            nc.sync.dma_start(out=raw[:], in_=x_rows[:, :, s % STEPS * TILE : (s % STEPS + 1) * TILE])
+            raw_tiles.append(raw)
+
+        load_step(0)
+
         w_plane = keep.tile([P, 2 * CHANNELS], U8, align_bytes=64)
         nc.vector.memset(w_plane[:].bitcast(I32), 0)
         for quad in range(4):
@@ -43,21 +58,18 @@ def tile_hydraattention_pa_t_kernel(tc, x, mask, w_words, w_scales, b_kv, out_kn
         w_codes = keep.tile([P, 2 * 2 * CHANNELS], U8, align_bytes=64)
         nc.sync.dma_start(out=w_codes[:].bitcast(I32), in_=w_words[0].bitcast(I32))
 
-        m_bc = keep.tile([P, IMAGES, PIXELS], BF16)
         bias_rows = keep.tile([P, P], BF16)
         nc.vector.memset(bias_rows[:], 0.0)
         nc.sync.dma_start(out=bias_rows[0 : 2 * CHUNKS, :], in_=b_kv.rearrange("(r c) -> r c", c=P))
-        raw_tiles = []
-        for b in range(IMAGES):
-            x_rows = x[b].rearrange("(p j) h w -> p j (h w)", j=PACK)
-            for step in range(STEPS):
-                raw = keep.tile([P, PACK, TILE], BF16, name="raw%d" % len(raw_tiles))
-                nc.sync.dma_start(out=raw[:], in_=x_rows[:, :, step * TILE : (step + 1) * TILE])
-                raw_tiles.append(raw)
-                if step == 1:
-                    nc.sync.dma_start(
-                        out=m_bc[:, b, :], in_=mask[b, 0].rearrange("h w -> (h w)").partition_broadcast(P)
-                    )
+
+        m_bc = keep.tile([P, IMAGES, PIXELS], BF16)
+        for s in range(1, STEPS_ALL):
+            load_step(s)
+            if s % STEPS == 1:
+                nc.sync.dma_start(
+                    out=m_bc[:, s // STEPS, :],
+                    in_=mask[s // STEPS, 0].rearrange("h w -> (h w)").partition_broadcast(P),
+                )
 
         ident_bf = keep.tile([P, P], BF16)
         make_identity(nc, ident_bf[:])
@@ -65,20 +77,17 @@ def tile_hydraattention_pa_t_kernel(tc, x, mask, w_words, w_scales, b_kv, out_kn
         make_identity(nc, ident_f32[:])
         ones = keep.tile([P, P], F32)
         nc.vector.memset(ones[:], 1.0)
+        table_warmer = keep.tile([P, 1], F32)
+        nc.scalar.activation(out=table_warmer[:], in_=ones[:, 0:1], func=ACT.Abs_reciprocal_sqrt)
         first_row = keep.tile([P, P], BF16)
         nc.vector.memset(first_row[:], 0.0)
         nc.vector.memset(first_row[0:1, :], 1.0)
         result = keep.tile([P, P], F32)
         nc.vector.memset(result[:], 0.0)
 
-        bias_ps = psum.tile([P, P], BF16, name="bias_ps", tag="norm")
-        nc.tensor.transpose(bias_ps[:], bias_rows[:], ident_bf[:])
-        bias = keep.tile([P, 2 * CHUNKS], F32)
-        nc.vector.tensor_copy(out=bias[:], in_=bias_ps[:, 0 : 2 * CHUNKS])
-
-        sums_all = keep.tile([P, IMAGES * CHUNKS, STEPS], F32)
-        sums_mask_v = keep.tile([P, IMAGES, VECTOR_CHUNKS, STEPS], F32)
-        sums_mask_s = keep.tile([P, IMAGES, CHUNKS - VECTOR_CHUNKS, STEPS], F32)
+        sums_all = keep.tile([P, IMAGES, CHUNKS, STEPS], F32)
+        sums_mask_s = keep.tile([P, IMAGES, GPSIMD_CHUNKS, STEPS], F32)
+        sums_mask_v = keep.tile([P, IMAGES, CHUNKS - GPSIMD_CHUNKS, STEPS], F32)
 
         grouped_of = {}
         codes_of = {}
@@ -87,8 +96,8 @@ def tile_hydraattention_pa_t_kernel(tc, x, mask, w_words, w_scales, b_kv, out_kn
         inv_norm_of = {}
         banks = {}
         mask_of = {}
-        weighted_of = {}
         khats_of = {}
+        weighted_of = {}
 
         def regroup(s, copy):
             if s >= STEPS_ALL:
@@ -103,8 +112,12 @@ def tile_hydraattention_pa_t_kernel(tc, x, mask, w_words, w_scales, b_kv, out_kn
         def quantise(s):
             if s >= STEPS_ALL:
                 return
-            x_codes = work.tile([P, TILE], U32, name="x_codes", tag="x_codes", bufs=5, align_bytes=64)
-            x_plane = work.tile([P, TILE], U8, name="x_plane", tag="x_plane", bufs=5, align_bytes=64)
+            x_codes = work.tile(
+                [P, TILE], U32, name="x_codes", tag="x_codes", bufs=QUANTISE_AHEAD + 2, align_bytes=64
+            )
+            x_plane = work.tile(
+                [P, TILE], U8, name="x_plane", tag="x_plane", bufs=QUANTISE_AHEAD + 2, align_bytes=64
+            )
             nc.vector.quantize_mx(
                 out=x_codes[:].bitcast(FP8X4),
                 scales=x_plane[:],
@@ -112,12 +125,12 @@ def tile_hydraattention_pa_t_kernel(tc, x, mask, w_words, w_scales, b_kv, out_kn
             )
             codes_of[s] = (x_codes, x_plane)
 
-        def project(acc, s, column_chunk):
+        def project(acc, s, w_chunk):
             x_codes, x_plane = codes_of[s]
             nc.tensor.matmul_mx(
                 out=acc[:],
-                lhsT=w_codes[:, 2 * P * column_chunk : 2 * P * (column_chunk + 1)].bitcast(FP4X4),
-                lhsT_scale=w_plane[:, P * column_chunk : P * (column_chunk + 1)],
+                lhsT=w_codes[:, 2 * P * w_chunk : 2 * P * (w_chunk + 1)].bitcast(FP4X4),
+                lhsT_scale=w_plane[:, P * w_chunk : P * (w_chunk + 1)],
                 rhs=x_codes[:].bitcast(FP8X4),
                 rhs_scale=x_plane[:],
                 start=True,
@@ -127,16 +140,16 @@ def tile_hydraattention_pa_t_kernel(tc, x, mask, w_words, w_scales, b_kv, out_kn
         def square_key(s, chunk):
             if s >= STEPS_ALL:
                 return
-            key = psum.tile([P, TILE], F32, name="key", tag="key", bufs=2)
+            key = psum.tile([P, TILE], F32, name="key", tag="key", bufs=KEY_BANKS)
             project(key, s, chunk)
-            square = work.tile([P, TILE], F32, name="square", tag="square", bufs=4)
+            square = work.tile([P, TILE], F32, name="square", tag="square", bufs=CHUNKS)
             nc.scalar.activation(
                 out=square[:], in_=key[:], func=ACT.Square, bias=bias[:, chunk : chunk + 1], scale=1.0
             )
             if chunk % 2 == 0:
                 pairs_of[s] = pairs_of.get(s, []) + [square]
             else:
-                pair = work.tile([P, TILE], F32, name="pair", tag="pair", bufs=6)
+                pair = work.tile([P, TILE], F32, name="pair", tag="pair", bufs=HALVES * (NORM_AHEAD + 1))
                 nc.gpsimd.tensor_tensor(out=pair[:], in0=pairs_of[s][-1][:], in1=square[:], op=ALU.add)
                 pairs_of[s][-1] = pair
 
@@ -146,15 +159,16 @@ def tile_hydraattention_pa_t_kernel(tc, x, mask, w_words, w_scales, b_kv, out_kn
             if half == 0:
                 norm_of[s] = psum.tile([P, TILE], F32, name="norm", tag="norm")
             nc.tensor.matmul(
-                out=norm_of[s][:], lhsT=ones[:], rhs=pairs_of[s][half][:], start=(half == 0), stop=(half == 1)
+                out=norm_of[s][:],
+                lhsT=ones[:],
+                rhs=pairs_of[s][half][:],
+                start=(half == 0),
+                stop=(half == HALVES - 1),
             )
-
-        def invert_norm(s):
-            if s >= STEPS_ALL:
-                return
-            inv_norm = work.tile([P, TILE], F32, name="inv_norm", tag="inv_norm", bufs=3)
-            nc.scalar.activation(out=inv_norm[:], in_=norm_of[s][:], func=ACT.Abs_reciprocal_sqrt)
-            inv_norm_of[s] = inv_norm
+            if half == HALVES - 1:
+                inv_norm = work.tile([P, TILE], F32, name="inv_norm", tag="inv_norm", bufs=NORM_AHEAD + 1)
+                nc.scalar.activation(out=inv_norm[:], in_=norm_of[s][:], func=ACT.Abs_reciprocal_sqrt)
+                inv_norm_of[s] = inv_norm
 
         def spread_mask(s):
             if s >= STEPS_ALL:
@@ -178,34 +192,41 @@ def tile_hydraattention_pa_t_kernel(tc, x, mask, w_words, w_scales, b_kv, out_kn
             banks[n] = bank
 
         def khat_pass(s, chunk):
+            n = 2 * CHUNKS * s + chunk
             khat = work.tile([P, TILE], F32, name="khat", tag="khat", bufs=CHUNKS)
             nc.vector.scalar_tensor_tensor(
                 out=khat[:],
-                in0=banks[2 * CHUNKS * s + chunk][:],
+                in0=banks[n][:],
                 scalar=bias[:, chunk : chunk + 1],
                 in1=inv_norm_of[s][:],
                 op0=ALU.add,
                 op1=ALU.mult,
             )
             khats_of[(s, chunk)] = khat
-            feed(2 * CHUNKS * s + chunk + AHEAD)
+            feed(n + AHEAD)
 
         def pool_pixels(s, chunk):
+            n = 2 * CHUNKS * s + CHUNKS + chunk
             b = s // STEPS
             step = s % STEPS
-            column = b * CHUNKS + chunk
-            product = work.tile([P, TILE], F32, name="product", tag="product", bufs=5)
+            product = work.tile([P, TILE], F32, name="product", tag="product", bufs=CHUNKS + 1)
             nc.vector.scalar_tensor_tensor(
                 out=product[:],
-                in0=banks[2 * CHUNKS * s + CHUNKS + chunk][:],
+                in0=banks[n][:],
                 scalar=bias[:, CHUNKS + chunk : CHUNKS + chunk + 1],
                 in1=khats_of[(s, chunk)][:],
                 op0=ALU.add,
                 op1=ALU.mult,
-                accum_out=sums_all[:, column, step : step + 1],
+                accum_out=sums_all[:, b, chunk, step : step + 1],
             )
-            feed(2 * CHUNKS * s + CHUNKS + chunk + AHEAD)
-            if chunk < VECTOR_CHUNKS:
+            feed(n + AHEAD)
+            if chunk < GPSIMD_CHUNKS:
+                weighted = work.tile([P, TILE], F32, name="weighted", tag="weighted", bufs=3 * GPSIMD_CHUNKS)
+                nc.gpsimd.tensor_tensor(
+                    out=weighted[:], in0=product[:], in1=m_bc[:, b, step * TILE : (step + 1) * TILE], op=ALU.mult
+                )
+                weighted_of[(s, chunk)] = weighted
+            else:
                 unused = work.tile([P, TILE], F32, name="unused", tag="unused", bufs=2)
                 nc.vector.scalar_tensor_tensor(
                     out=unused[:],
@@ -214,70 +235,70 @@ def tile_hydraattention_pa_t_kernel(tc, x, mask, w_words, w_scales, b_kv, out_kn
                     in1=product[:],
                     op0=ALU.mult,
                     op1=ALU.mult,
-                    accum_out=sums_mask_v[:, b, chunk, step : step + 1],
+                    accum_out=sums_mask_v[:, b, chunk - GPSIMD_CHUNKS, step : step + 1],
                 )
-            else:
-                weighted = work.tile([P, TILE], F32, name="weighted", tag="weighted", bufs=6)
-                nc.gpsimd.tensor_tensor(
-                    out=weighted[:], in0=product[:], in1=m_bc[:, b, step * TILE : (step + 1) * TILE], op=ALU.mult
-                )
-                weighted_of[(s, chunk)] = weighted
 
         def sum_weighted(s):
             if s < 0:
                 return
-            for chunk in range(VECTOR_CHUNKS, CHUNKS):
+            for chunk in range(GPSIMD_CHUNKS):
                 unread = work.tile([P, TILE], BF16, name="unread", tag="unread", bufs=2)
                 nc.scalar.activation(
                     out=unread[:],
                     in_=weighted_of[(s, chunk)][:],
                     func=ACT.Copy,
-                    accum_out=sums_mask_s[:, s // STEPS, chunk - VECTOR_CHUNKS, s % STEPS : s % STEPS + 1],
+                    accum_out=sums_mask_s[:, s // STEPS, chunk, s % STEPS : s % STEPS + 1],
                 )
 
-        for s in range(4):
+        regroup(0, nc.vector.tensor_copy)
+        quantise(0)
+
+        bias_ps = psum.tile([P, P], BF16, name="bias_ps", tag="norm")
+        nc.tensor.transpose(bias_ps[:], bias_rows[:], ident_bf[:])
+        bias = keep.tile([P, 2 * CHUNKS], F32)
+        nc.vector.tensor_copy(out=bias[:], in_=bias_ps[:, 0 : 2 * CHUNKS])
+
+        for s in range(1, REGROUP_AHEAD):
             regroup(s, nc.vector.tensor_copy)
-            if s < 3:
+            if s < QUANTISE_AHEAD:
                 quantise(s)
         for chunk in range(CHUNKS):
             square_key(0, chunk)
-        norm_pass(0, 0)
-        norm_pass(0, 1)
-        invert_norm(0)
-        for chunk in range(CHUNKS):
-            square_key(1, chunk)
-        norm_pass(1, 0)
-        norm_pass(1, 1)
-        invert_norm(1)
+        for half in range(HALVES):
+            norm_pass(0, half)
         spread_mask(0)
         for n in range(AHEAD):
             feed(n)
+        for chunk in range(CHUNKS):
+            square_key(1, chunk)
 
         for s in range(STEPS_ALL):
             for chunk in range(CHUNKS):
                 khat_pass(s, chunk)
-                square_key(s + 2, chunk)
-            quantise(s + 3)
-            regroup(s + 4, nc.scalar.copy)
+                square_key(s + NORM_AHEAD, chunk)
+            quantise(s + QUANTISE_AHEAD)
+            regroup(s + REGROUP_AHEAD, nc.scalar.copy)
             sum_weighted(s - 1)
+            norms_due = range(1, NORM_AHEAD + 1) if s == 0 else range(s + NORM_AHEAD, s + NORM_AHEAD + 1)
+            passes_due = [(late, half) for late in norms_due for half in range(HALVES)]
             for chunk in range(CHUNKS):
                 pool_pixels(s, chunk)
-                if chunk < 2:
-                    norm_pass(s + 2, chunk)
-                if chunk == 1:
-                    invert_norm(s + 2)
+                if chunk < len(passes_due):
+                    norm_pass(passes_due[chunk][0], passes_due[chunk][1])
             spread_mask(s + 1)
-
         sum_weighted(STEPS_ALL - 1)
+
         groups = IMAGES * CHUNKS
         total = keep.tile([P, groups], F32)
-        nc.vector.tensor_reduce(out=total[:], in_=sums_all[:], axis=mybir.AxisListType.X, op=ALU.add)
+        nc.vector.tensor_reduce(
+            out=total[:].rearrange("p (b c) -> p b c", b=IMAGES), in_=sums_all[:], axis=mybir.AxisListType.X, op=ALU.add
+        )
         masked = result[:, groups : 2 * groups].rearrange("p (b c) -> p b c", b=IMAGES)
         nc.vector.tensor_reduce(
-            out=masked[:, :, 0:VECTOR_CHUNKS], in_=sums_mask_v[:], axis=mybir.AxisListType.X, op=ALU.add
+            out=masked[:, :, 0:GPSIMD_CHUNKS], in_=sums_mask_s[:], axis=mybir.AxisListType.X, op=ALU.add
         )
         nc.vector.tensor_reduce(
-            out=masked[:, :, VECTOR_CHUNKS:CHUNKS], in_=sums_mask_s[:], axis=mybir.AxisListType.X, op=ALU.add
+            out=masked[:, :, GPSIMD_CHUNKS:CHUNKS], in_=sums_mask_v[:], axis=mybir.AxisListType.X, op=ALU.add
         )
         nc.vector.tensor_tensor(
             out=result[:, 0:groups], in0=total[:], in1=result[:, groups : 2 * groups], op=ALU.subtract

@@ -97,6 +97,7 @@ def tile_hydraattention_pa_t_kernel(tc, x, mask, w_words, w_scales, b_kv, out_kn
         banks = {}
         mask_of = {}
         khats_of = {}
+        products_of = {}
         weighted_of = {}
 
         def regroup(s, copy):
@@ -227,16 +228,19 @@ def tile_hydraattention_pa_t_kernel(tc, x, mask, w_words, w_scales, b_kv, out_kn
                 )
                 weighted_of[(s, chunk)] = weighted
             else:
-                unused = work.tile([P, TILE], F32, name="unused", tag="unused", bufs=2)
-                nc.vector.scalar_tensor_tensor(
-                    out=unused[:],
-                    in0=mask_of[s][:],
-                    scalar=1.0,
-                    in1=product[:],
-                    op0=ALU.mult,
-                    op1=ALU.mult,
-                    accum_out=sums_mask_v[:, b, chunk - GPSIMD_CHUNKS, step : step + 1],
-                )
+                products_of[(s, chunk)] = product
+
+        def weigh_on_vector(s, chunk):
+            unused = work.tile([P, TILE], F32, name="unused", tag="unused", bufs=2)
+            nc.vector.scalar_tensor_tensor(
+                out=unused[:],
+                in0=mask_of[s][:],
+                scalar=1.0,
+                in1=products_of[(s, chunk)][:],
+                op0=ALU.mult,
+                op1=ALU.mult,
+                accum_out=sums_mask_v[:, s // STEPS, chunk - GPSIMD_CHUNKS, s % STEPS : s % STEPS + 1],
+            )
 
         def sum_weighted(s):
             if s < 0:
@@ -285,6 +289,8 @@ def tile_hydraattention_pa_t_kernel(tc, x, mask, w_words, w_scales, b_kv, out_kn
                 pool_pixels(s, chunk)
                 if chunk < len(passes_due):
                     norm_pass(passes_due[chunk][0], passes_due[chunk][1])
+            for chunk in range(GPSIMD_CHUNKS, CHUNKS):
+                weigh_on_vector(s, chunk)
             spread_mask(s + 1)
         sum_weighted(STEPS_ALL - 1)
 

@@ -19,18 +19,19 @@ IMAGES = 2
 PIXELS = 4096
 CHANNELS = 512
 CHUNKS = CHANNELS // P
-TILE = 512
-STEPS = PIXELS // TILE
-STEPS_ALL = IMAGES * STEPS
-HALVES = 2
-GPSIMD_CHUNKS = 2
+TILES = IMAGES * PIXELS // P
+STEP = 4
+STEPS = TILES // STEP
+STEPS_IMAGE = STEPS // IMAGES
+STEP_PIXELS = STEP * P
+WEIGHTS = 2
 
-KEY_BANKS = 2
-AHEAD = 8 - KEY_BANKS - 2
+BANKS = 7
 
-NORM_AHEAD = 2
-QUANTISE_AHEAD = 3
-REGROUP_AHEAD = 4
+QUANTISE_AHEAD = 2
+REGROUP_AHEAD = 3
+FEED_AHEAD = 3
+SUM_LATE = 6
 
 
 def tile_hydraattention_pa_t_kernel(tc, x, mask, w_words, w_scales, b_kv, out_know, out_mask):
@@ -41,9 +42,10 @@ def tile_hydraattention_pa_t_kernel(tc, x, mask, w_words, w_scales, b_kv, out_kn
         raw_tiles = []
 
         def load_step(s):
-            x_rows = x[s // STEPS].rearrange("(p j) h w -> p j (h w)", j=PACK)
-            raw = keep.tile([P, PACK, TILE], BF16, name="raw%d" % s)
-            nc.sync.dma_start(out=raw[:], in_=x_rows[:, :, s % STEPS * TILE : (s % STEPS + 1) * TILE])
+            x_rows = x[s // STEPS_IMAGE].rearrange("(p j) h w -> p j (h w)", j=PACK)
+            raw = keep.tile([P, PACK, STEP_PIXELS], BF16, name="raw%d" % s)
+            first = s % STEPS_IMAGE * STEP_PIXELS
+            nc.sync.dma_start(out=raw[:], in_=x_rows[:, :, first : first + STEP_PIXELS])
             raw_tiles.append(raw)
 
         load_step(0)
@@ -58,66 +60,61 @@ def tile_hydraattention_pa_t_kernel(tc, x, mask, w_words, w_scales, b_kv, out_kn
         w_codes = keep.tile([P, 2 * 2 * CHANNELS], U8, align_bytes=64)
         nc.sync.dma_start(out=w_codes[:].bitcast(I32), in_=w_words[0].bitcast(I32))
 
-        bias_rows = keep.tile([P, P], BF16)
-        nc.vector.memset(bias_rows[:], 0.0)
-        nc.sync.dma_start(out=bias_rows[0 : 2 * CHUNKS, :], in_=b_kv.rearrange("(r c) -> r c", c=P))
-
-        m_bc = keep.tile([P, IMAGES, PIXELS], BF16)
-        for s in range(1, STEPS_ALL):
+        bias_row = keep.tile([P, 2 * CHANNELS], BF16)
+        nc.gpsimd.memset(bias_row[:], 0.0)
+        nc.sync.dma_start(out=bias_row[0:1, :], in_=b_kv.rearrange("(r c) -> r c", r=1))
+        mask_rows = keep.tile([P, P], BF16)
+        nc.gpsimd.memset(mask_rows[:], 0.0)
+        for s in range(1, STEPS):
             load_step(s)
-            if s % STEPS == 1:
+            if s == 1:
                 nc.sync.dma_start(
-                    out=m_bc[:, s // STEPS, :],
-                    in_=mask[s // STEPS, 0].rearrange("h w -> (h w)").partition_broadcast(P),
+                    out=mask_rows[0:TILES, :], in_=mask.rearrange("b o (t r) w -> (b o t) (r w)", r=2)
                 )
 
         ident_bf = keep.tile([P, P], BF16)
         make_identity(nc, ident_bf[:])
         ident_f32 = keep.tile([P, P], F32)
         make_identity(nc, ident_f32[:])
-        ones = keep.tile([P, P], F32)
+        ones = keep.tile([P, P], BF16)
         nc.vector.memset(ones[:], 1.0)
         table_warmer = keep.tile([P, 1], F32)
         nc.scalar.activation(out=table_warmer[:], in_=ones[:, 0:1], func=ACT.Abs_reciprocal_sqrt)
-        first_row = keep.tile([P, P], BF16)
-        nc.vector.memset(first_row[:], 0.0)
-        nc.vector.memset(first_row[0:1, :], 1.0)
         result = keep.tile([P, P], F32)
-        nc.vector.memset(result[:], 0.0)
+        nc.gpsimd.memset(result[:], 0.0)
 
-        sums_all = keep.tile([P, IMAGES, CHUNKS, STEPS], F32)
-        sums_mask_s = keep.tile([P, IMAGES, GPSIMD_CHUNKS, STEPS], F32)
-        sums_mask_v = keep.tile([P, IMAGES, CHUNKS - GPSIMD_CHUNKS, STEPS], F32)
+        square_sums = keep.tile([P, TILES], F32)
+        weights = keep.tile([P, TILES, WEIGHTS], F32)
+        sums_ps = psum.tile([P, IMAGES, CHUNKS, TILES // IMAGES, WEIGHTS], F32)
 
         grouped_of = {}
         codes_of = {}
-        pairs_of = {}
-        norm_of = {}
-        inv_norm_of = {}
         banks = {}
-        mask_of = {}
-        khats_of = {}
+        keys_of = {}
+        values_of = {}
         products_of = {}
-        weighted_of = {}
 
-        def regroup(s, copy):
-            if s >= STEPS_ALL:
+        def regroup(s, part, copy):
+            if s >= STEPS:
                 return
-            grouped = work.tile([P, TILE, PACK], BF16, name="grouped", tag="grouped", bufs=3, align_bytes=64)
+            if part == 0:
+                grouped_of[s] = work.tile(
+                    [P, STEP_PIXELS, PACK], BF16, name="grouped", tag="grouped", bufs=3, align_bytes=64
+                )
+            here = slice(part * P, (part + 1) * P)
             copy(
-                out=grouped[:].rearrange("p (c i) j -> p c j i", i=4),
-                in_=raw_tiles[s][:].rearrange("p j (c i) -> p c j i", i=4),
+                out=grouped_of[s][:, here, :].rearrange("p (c i) j -> p c j i", i=4),
+                in_=raw_tiles[s][:, :, here].rearrange("p j (c i) -> p c j i", i=4),
             )
-            grouped_of[s] = grouped
 
         def quantise(s):
-            if s >= STEPS_ALL:
+            if s >= STEPS:
                 return
             x_codes = work.tile(
-                [P, TILE], U32, name="x_codes", tag="x_codes", bufs=QUANTISE_AHEAD + 2, align_bytes=64
+                [P, STEP_PIXELS], U32, name="x_codes", tag="x_codes", bufs=QUANTISE_AHEAD + 2, align_bytes=64
             )
             x_plane = work.tile(
-                [P, TILE], U8, name="x_plane", tag="x_plane", bufs=QUANTISE_AHEAD + 2, align_bytes=64
+                [P, STEP_PIXELS], U8, name="x_plane", tag="x_plane", bufs=QUANTISE_AHEAD + 2, align_bytes=64
             )
             nc.vector.quantize_mx(
                 out=x_codes[:].bitcast(FP8X4),
@@ -126,190 +123,119 @@ def tile_hydraattention_pa_t_kernel(tc, x, mask, w_words, w_scales, b_kv, out_kn
             )
             codes_of[s] = (x_codes, x_plane)
 
-        def project(acc, s, w_chunk):
-            x_codes, x_plane = codes_of[s]
+        def feed(i, side):
+            if i >= TILES:
+                return
+            x_codes, x_plane = codes_of[i // STEP]
+            here = slice(i % STEP * P, (i % STEP + 1) * P)
+            bank = psum.tile([P, CHANNELS], F32, name="bank", tag="bank", bufs=BANKS)
             nc.tensor.matmul_mx(
-                out=acc[:],
-                lhsT=w_codes[:, 2 * P * w_chunk : 2 * P * (w_chunk + 1)].bitcast(FP4X4),
-                lhsT_scale=w_plane[:, P * w_chunk : P * (w_chunk + 1)],
-                rhs=x_codes[:].bitcast(FP8X4),
-                rhs_scale=x_plane[:],
+                out=bank[:],
+                lhsT=x_codes[:, here].bitcast(FP8X4),
+                lhsT_scale=x_plane[:, here],
+                rhs=w_codes[:, 2 * CHANNELS * side : 2 * CHANNELS * (side + 1)].bitcast(FP4X4),
+                rhs_scale=w_plane[:, CHANNELS * side : CHANNELS * (side + 1)],
                 start=True,
                 stop=True,
             )
+            banks[(i, side)] = bank
 
-        def square_key(s, chunk):
-            if s >= STEPS_ALL:
-                return
-            key = psum.tile([P, TILE], F32, name="key", tag="key", bufs=KEY_BANKS)
-            project(key, s, chunk)
-            square = work.tile([P, TILE], F32, name="square", tag="square", bufs=CHUNKS)
+        def add_bias(i, side):
+            out = work.tile([P, CHANNELS], F32, name="keyval", tag="key" if side == 0 else "value", bufs=4)
+            nc.vector.tensor_tensor(
+                out=out[:],
+                in0=banks[(i, side)][:],
+                in1=bias[:, CHANNELS * side : CHANNELS * (side + 1)],
+                op=ALU.add,
+            )
+            return out
+
+        def square_key(i):
+            unread = work.tile([P, CHANNELS], BF16, name="unread", tag="unread", bufs=2)
             nc.scalar.activation(
-                out=square[:], in_=key[:], func=ACT.Square, bias=bias[:, chunk : chunk + 1], scale=1.0
+                out=unread[:], in_=keys_of[i][:], func=ACT.Square, accum_out=square_sums[:, i : i + 1]
             )
-            if chunk % 2 == 0:
-                pairs_of[s] = pairs_of.get(s, []) + [square]
-            else:
-                pair = work.tile([P, TILE], F32, name="pair", tag="pair", bufs=HALVES * (NORM_AHEAD + 1))
-                nc.gpsimd.tensor_tensor(out=pair[:], in0=pairs_of[s][-1][:], in1=square[:], op=ALU.add)
-                pairs_of[s][-1] = pair
 
-        def norm_pass(s, half):
-            if s >= STEPS_ALL:
-                return
-            if half == 0:
-                norm_of[s] = psum.tile([P, TILE], F32, name="norm", tag="norm")
-            nc.tensor.matmul(
-                out=norm_of[s][:],
-                lhsT=ones[:],
-                rhs=pairs_of[s][half][:],
-                start=(half == 0),
-                stop=(half == HALVES - 1),
+        def multiply(i):
+            product = work.tile([P, CHANNELS], F32, name="product", tag="product", bufs=SUM_LATE + 4)
+            nc.gpsimd.tensor_tensor(out=product[:], in0=keys_of[i][:], in1=values_of[i][:], op=ALU.mult)
+            products_of[i] = product
+
+        def weigh(s):
+            tiles = slice(s * STEP, (s + 1) * STEP)
+            nc.scalar.activation(
+                out=weights[:, tiles, 0], in_=square_sums[:, tiles], func=ACT.Abs_reciprocal_sqrt
             )
-            if half == HALVES - 1:
-                inv_norm = work.tile([P, TILE], F32, name="inv_norm", tag="inv_norm", bufs=NORM_AHEAD + 1)
-                nc.scalar.activation(out=inv_norm[:], in_=norm_of[s][:], func=ACT.Abs_reciprocal_sqrt)
-                inv_norm_of[s] = inv_norm
+            nc.gpsimd.tensor_tensor(
+                out=weights[:, tiles, 1], in0=weights[:, tiles, 0], in1=m_col[:, tiles], op=ALU.mult
+            )
 
-        def spread_mask(s):
-            if s >= STEPS_ALL:
+        def sum_pixels(i, chunk):
+            if i < 0:
                 return
-            mask_ps = psum.tile([P, TILE], F32, name="mask_ps", tag="mask_ps")
             nc.tensor.matmul(
-                out=mask_ps[:],
-                lhsT=first_row[:],
-                rhs=m_bc[:, s // STEPS, s % STEPS * TILE : (s % STEPS + 1) * TILE],
+                out=sums_ps[:, i // (TILES // IMAGES), chunk, i % (TILES // IMAGES), :],
+                lhsT=products_of[i][:, chunk * P : (chunk + 1) * P],
+                rhs=weights[:, i, :],
                 start=True,
                 stop=True,
             )
-            mask_of[s] = mask_ps
 
-        def feed(n):
-            s = n // (2 * CHUNKS)
-            if s >= STEPS_ALL:
-                return
-            bank = psum.tile([P, TILE], F32, name="bank", tag="bank", bufs=AHEAD)
-            project(bank, s, n % (2 * CHUNKS))
-            banks[n] = bank
-
-        def khat_pass(s, chunk):
-            n = 2 * CHUNKS * s + chunk
-            khat = work.tile([P, TILE], F32, name="khat", tag="khat", bufs=CHUNKS)
-            nc.vector.scalar_tensor_tensor(
-                out=khat[:],
-                in0=banks[n][:],
-                scalar=bias[:, chunk : chunk + 1],
-                in1=inv_norm_of[s][:],
-                op0=ALU.add,
-                op1=ALU.mult,
-            )
-            khats_of[(s, chunk)] = khat
-            feed(n + AHEAD)
-
-        def pool_pixels(s, chunk):
-            n = 2 * CHUNKS * s + CHUNKS + chunk
-            b = s // STEPS
-            step = s % STEPS
-            product = work.tile([P, TILE], F32, name="product", tag="product", bufs=CHUNKS + 1)
-            nc.vector.scalar_tensor_tensor(
-                out=product[:],
-                in0=banks[n][:],
-                scalar=bias[:, CHUNKS + chunk : CHUNKS + chunk + 1],
-                in1=khats_of[(s, chunk)][:],
-                op0=ALU.add,
-                op1=ALU.mult,
-                accum_out=sums_all[:, b, chunk, step : step + 1],
-            )
-            feed(n + AHEAD)
-            if chunk < GPSIMD_CHUNKS:
-                weighted = work.tile([P, TILE], F32, name="weighted", tag="weighted", bufs=3 * GPSIMD_CHUNKS)
-                nc.gpsimd.tensor_tensor(
-                    out=weighted[:], in0=product[:], in1=m_bc[:, b, step * TILE : (step + 1) * TILE], op=ALU.mult
-                )
-                weighted_of[(s, chunk)] = weighted
-            else:
-                products_of[(s, chunk)] = product
-
-        def weigh_on_vector(s, chunk):
-            unused = work.tile([P, TILE], F32, name="unused", tag="unused", bufs=2)
-            nc.vector.scalar_tensor_tensor(
-                out=unused[:],
-                in0=mask_of[s][:],
-                scalar=1.0,
-                in1=products_of[(s, chunk)][:],
-                op0=ALU.mult,
-                op1=ALU.mult,
-                accum_out=sums_mask_v[:, s // STEPS, chunk - GPSIMD_CHUNKS, s % STEPS : s % STEPS + 1],
-            )
-
-        def sum_weighted(s):
-            if s < 0:
-                return
-            for chunk in range(GPSIMD_CHUNKS):
-                unread = work.tile([P, TILE], BF16, name="unread", tag="unread", bufs=2)
-                nc.scalar.activation(
-                    out=unread[:],
-                    in_=weighted_of[(s, chunk)][:],
-                    func=ACT.Copy,
-                    accum_out=sums_mask_s[:, s // STEPS, chunk, s % STEPS : s % STEPS + 1],
-                )
-
-        regroup(0, nc.vector.tensor_copy)
+        for part in range(STEP):
+            regroup(0, part, nc.vector.tensor_copy)
         quantise(0)
+        bias = keep.tile([P, 2 * CHANNELS], F32)
+        for side in range(2):
+            bias_ps = psum.tile([P, CHANNELS], F32, name="bank", tag="bank", bufs=BANKS)
+            here = slice(CHANNELS * side, CHANNELS * (side + 1))
+            nc.tensor.matmul(out=bias_ps[:], lhsT=ones[:], rhs=bias_row[:, here], start=True, stop=True)
+            nc.scalar.copy(out=bias[:, here], in_=bias_ps[:])
+        for i in range(FEED_AHEAD):
+            feed(i, 0)
+            feed(i, 1)
+        mask_ps = psum.tile([P, P], BF16, name="bank", tag="bank", bufs=BANKS)
+        nc.tensor.transpose(mask_ps[:], mask_rows[:], ident_bf[:])
+        m_col = keep.tile([P, TILES], F32)
+        nc.scalar.copy(out=m_col[:], in_=mask_ps[:, 0:TILES])
+        for part in range(STEP):
+            regroup(1, part, nc.vector.tensor_copy)
+        quantise(1)
+        for part in range(STEP):
+            regroup(2, part, nc.scalar.copy)
 
-        bias_ps = psum.tile([P, P], BF16, name="bias_ps", tag="norm")
-        nc.tensor.transpose(bias_ps[:], bias_rows[:], ident_bf[:])
-        bias = keep.tile([P, 2 * CHUNKS], F32)
-        nc.vector.tensor_copy(out=bias[:], in_=bias_ps[:, 0 : 2 * CHUNKS])
-
-        for s in range(1, REGROUP_AHEAD):
-            regroup(s, nc.vector.tensor_copy)
-            if s < QUANTISE_AHEAD:
-                quantise(s)
-        for chunk in range(CHUNKS):
-            square_key(0, chunk)
-        for half in range(HALVES):
-            norm_pass(0, half)
-        spread_mask(0)
-        for n in range(AHEAD):
-            feed(n)
-        for chunk in range(CHUNKS):
-            square_key(1, chunk)
-
-        for s in range(STEPS_ALL):
+        for i in range(TILES):
+            s = i // STEP
+            keys_of[i] = add_bias(i, 0)
+            square_key(i)
+            regroup(s + REGROUP_AHEAD, i % STEP, nc.scalar.copy)
+            if i % STEP == 0 and s > 0:
+                weigh(s - 1)
+            feed(i + FEED_AHEAD, 0)
+            for chunk in range(2):
+                sum_pixels(i - SUM_LATE, chunk)
+            values_of[i] = add_bias(i, 1)
+            multiply(i)
+            feed(i + FEED_AHEAD, 1)
+            for chunk in range(2, CHUNKS):
+                sum_pixels(i - SUM_LATE, chunk)
+            if i % STEP == 0:
+                quantise(s + QUANTISE_AHEAD)
+        weigh(STEPS - 1)
+        for i in range(TILES - SUM_LATE, TILES):
             for chunk in range(CHUNKS):
-                khat_pass(s, chunk)
-                square_key(s + NORM_AHEAD, chunk)
-            quantise(s + QUANTISE_AHEAD)
-            regroup(s + REGROUP_AHEAD, nc.scalar.copy)
-            sum_weighted(s - 1)
-            norms_due = range(1, NORM_AHEAD + 1) if s == 0 else range(s + NORM_AHEAD, s + NORM_AHEAD + 1)
-            passes_due = [(late, half) for late in norms_due for half in range(HALVES)]
-            for chunk in range(CHUNKS):
-                pool_pixels(s, chunk)
-                if chunk < len(passes_due):
-                    norm_pass(passes_due[chunk][0], passes_due[chunk][1])
-            for chunk in range(GPSIMD_CHUNKS, CHUNKS):
-                weigh_on_vector(s, chunk)
-            spread_mask(s + 1)
-        sum_weighted(STEPS_ALL - 1)
+                sum_pixels(i, chunk)
 
         groups = IMAGES * CHUNKS
-        total = keep.tile([P, groups], F32)
+        total = keep.tile([P, groups, WEIGHTS], F32)
         nc.vector.tensor_reduce(
-            out=total[:].rearrange("p (b c) -> p b c", b=IMAGES), in_=sums_all[:], axis=mybir.AxisListType.X, op=ALU.add
+            out=total[:],
+            in_=sums_ps[:].rearrange("p b c t w -> p (b c) w t"),
+            axis=mybir.AxisListType.X,
+            op=ALU.add,
         )
-        masked = result[:, groups : 2 * groups].rearrange("p (b c) -> p b c", b=IMAGES)
-        nc.vector.tensor_reduce(
-            out=masked[:, :, 0:GPSIMD_CHUNKS], in_=sums_mask_s[:], axis=mybir.AxisListType.X, op=ALU.add
-        )
-        nc.vector.tensor_reduce(
-            out=masked[:, :, GPSIMD_CHUNKS:CHUNKS], in_=sums_mask_v[:], axis=mybir.AxisListType.X, op=ALU.add
-        )
-        nc.vector.tensor_tensor(
-            out=result[:, 0:groups], in0=total[:], in1=result[:, groups : 2 * groups], op=ALU.subtract
-        )
-        rows_ps = psum.tile([P, P], F32, name="rows_ps", tag="norm")
+        nc.vector.tensor_copy(out=result[:, groups : 2 * groups], in_=total[:, :, 1])
+        nc.vector.tensor_tensor(out=result[:, 0:groups], in0=total[:, :, 0], in1=total[:, :, 1], op=ALU.subtract)
+        rows_ps = psum.tile([P, P], F32, name="bank", tag="bank", bufs=BANKS)
         nc.tensor.transpose(rows_ps[:], result[:], ident_f32[:])
         rows = keep.tile([2 * groups, P], F32)
         nc.scalar.copy(out=rows[:], in_=rows_ps[0 : 2 * groups, :])

@@ -31,7 +31,7 @@ BANKS = 7
 QUANTISE_AHEAD = 2
 REGROUP_AHEAD = 3
 FEED_AHEAD = 3
-SUM_LATE = 6
+SUM_LATE = 2
 
 
 def tile_hydraattention_pa_t_kernel(tc, x, mask, w_words, w_scales, b_kv, out_know, out_mask):
@@ -157,17 +157,18 @@ def tile_hydraattention_pa_t_kernel(tc, x, mask, w_words, w_scales, b_kv, out_kn
             )
 
         def multiply(i):
-            product = work.tile([P, CHANNELS], F32, name="product", tag="product", bufs=SUM_LATE + 4)
+            product = work.tile([P, CHANNELS], F32, name="product", tag="product", bufs=SUM_LATE + 3)
             nc.gpsimd.tensor_tensor(out=product[:], in0=keys_of[i][:], in1=values_of[i][:], op=ALU.mult)
             products_of[i] = product
 
-        def weigh(s):
-            tiles = slice(s * STEP, (s + 1) * STEP)
+        def invert_norm(i):
             nc.scalar.activation(
-                out=weights[:, tiles, 0], in_=square_sums[:, tiles], func=ACT.Abs_reciprocal_sqrt
+                out=weights[:, i, 0:1], in_=square_sums[:, i : i + 1], func=ACT.Abs_reciprocal_sqrt
             )
-            nc.gpsimd.tensor_tensor(
-                out=weights[:, tiles, 1], in0=weights[:, tiles, 0], in1=m_col[:, tiles], op=ALU.mult
+
+        def weigh_mask(i):
+            nc.scalar.activation(
+                out=weights[:, i, 1:2], in_=m_col[:, i : i + 1], func=ACT.Copy, scale=weights[:, i, 0:1]
             )
 
         def sum_pixels(i, chunk):
@@ -207,9 +208,11 @@ def tile_hydraattention_pa_t_kernel(tc, x, mask, w_words, w_scales, b_kv, out_kn
             s = i // STEP
             keys_of[i] = add_bias(i, 0)
             square_key(i)
+            if i > 0:
+                invert_norm(i - 1)
             regroup(s + REGROUP_AHEAD, i % STEP, nc.scalar.copy)
-            if i % STEP == 0 and s > 0:
-                weigh(s - 1)
+            if i > 0:
+                weigh_mask(i - 1)
             feed(i + FEED_AHEAD, 0)
             for chunk in range(2):
                 sum_pixels(i - SUM_LATE, chunk)
@@ -220,7 +223,8 @@ def tile_hydraattention_pa_t_kernel(tc, x, mask, w_words, w_scales, b_kv, out_kn
                 sum_pixels(i - SUM_LATE, chunk)
             if i % STEP == 0:
                 quantise(s + QUANTISE_AHEAD)
-        weigh(STEPS - 1)
+        invert_norm(TILES - 1)
+        weigh_mask(TILES - 1)
         for i in range(TILES - SUM_LATE, TILES):
             for chunk in range(CHUNKS):
                 sum_pixels(i, chunk)

@@ -32,6 +32,7 @@ QUANTISE_AHEAD = 2
 REGROUP_AHEAD = 3
 FEED_AHEAD = 3
 SUM_LATE = 2
+REPEATS = 16
 
 
 def tile_hydraattention_pa_t_kernel(tc, x, mask, w_words, w_scales, b_kv, out_know, out_mask):
@@ -85,7 +86,7 @@ def tile_hydraattention_pa_t_kernel(tc, x, mask, w_words, w_scales, b_kv, out_kn
 
         square_sums = keep.tile([P, TILES], F32)
         weights = keep.tile([P, TILES, WEIGHTS], F32)
-        sums_ps = psum.tile([P, IMAGES, CHUNKS, TILES // IMAGES, WEIGHTS], F32)
+        sums_ps = psum.tile([P, TILES * CHUNKS * WEIGHTS], F32)
 
         grouped_of = {}
         codes_of = {}
@@ -174,10 +175,12 @@ def tile_hydraattention_pa_t_kernel(tc, x, mask, w_words, w_scales, b_kv, out_kn
         def sum_pixels(i, chunk):
             if i < 0:
                 return
+            column = (i * CHUNKS + chunk) * WEIGHTS
+            repeats = min(REPEATS, TILES * CHUNKS - (i * CHUNKS + chunk))
             nc.tensor.matmul(
-                out=sums_ps[:, i // (TILES // IMAGES), chunk, i % (TILES // IMAGES), :],
+                out=sums_ps[:, column : column + repeats * WEIGHTS],
                 lhsT=products_of[i][:, chunk * P : (chunk + 1) * P],
-                rhs=weights[:, i, :],
+                rhs=weights[:, i, :].unsqueeze(1).to_broadcast([P, repeats, WEIGHTS]),
                 start=True,
                 stop=True,
             )
@@ -231,12 +234,14 @@ def tile_hydraattention_pa_t_kernel(tc, x, mask, w_words, w_scales, b_kv, out_kn
 
         groups = IMAGES * CHUNKS
         total = keep.tile([P, groups, WEIGHTS], F32)
-        nc.vector.tensor_reduce(
-            out=total[:],
-            in_=sums_ps[:].rearrange("p b c t w -> p (b c) w t"),
-            axis=mybir.AxisListType.X,
-            op=ALU.add,
-        )
+        width = TILES // IMAGES * CHUNKS * WEIGHTS
+        for b in range(IMAGES):
+            nc.vector.tensor_reduce(
+                out=total[:, b * CHUNKS : (b + 1) * CHUNKS, :],
+                in_=sums_ps[:, b * width : (b + 1) * width].rearrange("p (t c w) -> p c w t", c=CHUNKS, w=WEIGHTS),
+                axis=mybir.AxisListType.X,
+                op=ALU.add,
+            )
         nc.vector.tensor_copy(out=result[:, groups : 2 * groups], in_=total[:, :, 1])
         nc.vector.tensor_tensor(out=result[:, 0:groups], in0=total[:, :, 0], in1=total[:, :, 1], op=ALU.subtract)
         rows_ps = psum.tile([P, P], F32, name="bank", tag="bank", bufs=BANKS)

@@ -20,19 +20,23 @@ PIXELS = 4096
 CHANNELS = 512
 CHUNKS = CHANNELS // P
 TILES = IMAGES * PIXELS // P
+TILES_IMAGE = TILES // IMAGES
 STEP = 4
 STEPS = TILES // STEP
 STEPS_IMAGE = STEPS // IMAGES
 STEP_PIXELS = STEP * P
 WEIGHTS = 2
 
-BANKS = 7
+GROUPS = WEIGHTS * IMAGES * CHUNKS
 
-QUANTISE_AHEAD = 2
-REGROUP_AHEAD = 3
+BANKS = 6
+
+QUANTISE_AHEAD = 1
+REGROUP_AHEAD = 2
 FEED_AHEAD = 3
 SUM_LATE = 2
 REPEATS = 16
+REPEATS_LAST = 32
 
 
 def tile_hydraattention_pa_t_kernel(tc, x, mask, w_words, w_scales, b_kv, out_know, out_mask):
@@ -42,14 +46,20 @@ def tile_hydraattention_pa_t_kernel(tc, x, mask, w_words, w_scales, b_kv, out_kn
     ) as psum, tc.manual_schedule():
         raw_tiles = []
 
-        def load_step(s):
+        def load_step(s, pieces, queue=nc.sync):
             x_rows = x[s // STEPS_IMAGE].rearrange("(p j) h w -> p j (h w)", j=PACK)
-            raw = keep.tile([P, PACK, STEP_PIXELS], BF16, name="raw%d" % s)
+            if s == len(raw_tiles):
+                raw_tiles.append(keep.tile([P, PACK, STEP_PIXELS], BF16, name="raw%d" % s))
+            raw = raw_tiles[s]
             first = s % STEPS_IMAGE * STEP_PIXELS
-            nc.sync.dma_start(out=raw[:], in_=x_rows[:, :, first : first + STEP_PIXELS])
-            raw_tiles.append(raw)
+            for start, end in pieces:
+                queue.dma_start(out=raw[:, :, start:end], in_=x_rows[:, :, first + start : first + end])
 
-        load_step(0)
+        load_step(0, [(0, P)])
+        load_step(0, [(P, STEP_PIXELS)], nc.scalar)
+        table_warmer = keep.tile([P, 1], F32)
+        nc.vector.memset(table_warmer[:], 1.0)
+        nc.scalar.activation(out=table_warmer[:], in_=table_warmer[:], func=ACT.Abs_reciprocal_sqrt)
 
         w_plane = keep.tile([P, 2 * CHANNELS], U8, align_bytes=64)
         nc.vector.memset(w_plane[:].bitcast(I32), 0)
@@ -62,16 +72,13 @@ def tile_hydraattention_pa_t_kernel(tc, x, mask, w_words, w_scales, b_kv, out_kn
         nc.sync.dma_start(out=w_codes[:].bitcast(I32), in_=w_words[0].bitcast(I32))
 
         bias_row = keep.tile([P, 2 * CHANNELS], BF16)
-        nc.gpsimd.memset(bias_row[:], 0.0)
-        nc.sync.dma_start(out=bias_row[0:1, :], in_=b_kv.rearrange("(r c) -> r c", r=1))
+        nc.vector.memset(bias_row[:].bitcast(I32), 0)
+        nc.scalar.dma_start(out=bias_row[0:1, :], in_=b_kv.rearrange("(r c) -> r c", r=1))
         mask_rows = keep.tile([P, P], BF16)
-        nc.gpsimd.memset(mask_rows[:], 0.0)
+        nc.vector.memset(mask_rows[:], 0.0)
+        nc.scalar.dma_start(out=mask_rows[0:TILES, :], in_=mask.rearrange("b o (t r) w -> (b o t) (r w)", r=2))
         for s in range(1, STEPS):
-            load_step(s)
-            if s == 1:
-                nc.sync.dma_start(
-                    out=mask_rows[0:TILES, :], in_=mask.rearrange("b o (t r) w -> (b o t) (r w)", r=2)
-                )
+            load_step(s, [(0, STEP_PIXELS)])
 
         ident_bf = keep.tile([P, P], BF16)
         make_identity(nc, ident_bf[:])
@@ -79,14 +86,13 @@ def tile_hydraattention_pa_t_kernel(tc, x, mask, w_words, w_scales, b_kv, out_kn
         make_identity(nc, ident_f32[:])
         ones = keep.tile([P, P], BF16)
         nc.vector.memset(ones[:], 1.0)
-        table_warmer = keep.tile([P, 1], F32)
-        nc.scalar.activation(out=table_warmer[:], in_=ones[:, 0:1], func=ACT.Abs_reciprocal_sqrt)
         result = keep.tile([P, P], F32)
         nc.gpsimd.memset(result[:], 0.0)
 
         square_sums = keep.tile([P, TILES], F32)
+        inv_norm = keep.tile([P, TILES], F32)
         weights = keep.tile([P, TILES, WEIGHTS], F32)
-        sums_ps = psum.tile([P, TILES * CHUNKS * WEIGHTS], F32)
+        sums_ps = [psum.tile([P, 2, TILES_IMAGE, CHUNKS, WEIGHTS], F32, name="sums%d" % b) for b in range(IMAGES)]
 
         grouped_of = {}
         codes_of = {}
@@ -98,7 +104,7 @@ def tile_hydraattention_pa_t_kernel(tc, x, mask, w_words, w_scales, b_kv, out_kn
         def regroup(s, part, copy):
             if s >= STEPS:
                 return
-            if part == 0:
+            if s not in grouped_of:
                 grouped_of[s] = work.tile(
                     [P, STEP_PIXELS, PACK], BF16, name="grouped", tag="grouped", bufs=3, align_bytes=64
                 )
@@ -108,21 +114,24 @@ def tile_hydraattention_pa_t_kernel(tc, x, mask, w_words, w_scales, b_kv, out_kn
                 in_=raw_tiles[s][:, :, here].rearrange("p j (c i) -> p c j i", i=4),
             )
 
-        def quantise(s):
+        def quantise(s, first=0, tiles=STEP):
             if s >= STEPS:
                 return
-            x_codes = work.tile(
-                [P, STEP_PIXELS], U32, name="x_codes", tag="x_codes", bufs=QUANTISE_AHEAD + 2, align_bytes=64
-            )
-            x_plane = work.tile(
-                [P, STEP_PIXELS], U8, name="x_plane", tag="x_plane", bufs=QUANTISE_AHEAD + 2, align_bytes=64
-            )
+            if first == 0:
+                x_codes = work.tile(
+                    [P, STEP_PIXELS], U32, name="x_codes", tag="x_codes", bufs=QUANTISE_AHEAD + 2, align_bytes=64
+                )
+                x_plane = work.tile(
+                    [P, STEP_PIXELS], U8, name="x_plane", tag="x_plane", bufs=QUANTISE_AHEAD + 2, align_bytes=64
+                )
+                codes_of[s] = (x_codes, x_plane)
+            x_codes, x_plane = codes_of[s]
+            here = slice(first * P, (first + tiles) * P)
             nc.vector.quantize_mx(
-                out=x_codes[:].bitcast(FP8X4),
-                scales=x_plane[:],
-                in_=grouped_of[s][:].rearrange("p t j -> p (t j)"),
+                out=x_codes[:, here].bitcast(FP8X4),
+                scales=x_plane[:, here],
+                in_=grouped_of[s][:, here, :].rearrange("p t j -> p (t j)"),
             )
-            codes_of[s] = (x_codes, x_plane)
 
         def feed(i, side):
             if i >= TILES:
@@ -159,53 +168,73 @@ def tile_hydraattention_pa_t_kernel(tc, x, mask, w_words, w_scales, b_kv, out_kn
 
         def multiply(i):
             product = work.tile([P, CHANNELS], F32, name="product", tag="product", bufs=SUM_LATE + 3)
-            nc.gpsimd.tensor_tensor(out=product[:], in0=keys_of[i][:], in1=values_of[i][:], op=ALU.mult)
+            if i < TILES - 1:
+                nc.gpsimd.tensor_tensor(out=product[:], in0=keys_of[i][:], in1=values_of[i][:], op=ALU.mult)
+            else:
+                for half in range(2):
+                    here = slice(half * CHANNELS // 2, (half + 1) * CHANNELS // 2)
+                    nc.vector.tensor_tensor(
+                        out=product[:, here], in0=keys_of[i][:, here], in1=values_of[i][:, here], op=ALU.mult
+                    )
             products_of[i] = product
 
         def invert_norm(i):
             nc.scalar.activation(
-                out=weights[:, i, 0:1], in_=square_sums[:, i : i + 1], func=ACT.Abs_reciprocal_sqrt
+                out=inv_norm[:, i : i + 1], in_=square_sums[:, i : i + 1], func=ACT.Abs_reciprocal_sqrt
             )
 
-        def weigh_mask(i):
+        def weigh(i):
             nc.scalar.activation(
-                out=weights[:, i, 1:2], in_=m_col[:, i : i + 1], func=ACT.Copy, scale=weights[:, i, 0:1]
+                out=weights[:, i, :], in_=shares[:, i, :], func=ACT.Copy, scale=inv_norm[:, i : i + 1]
             )
 
         def sum_pixels(i, chunk):
             if i < 0:
                 return
-            column = (i * CHUNKS + chunk) * WEIGHTS
-            repeats = min(REPEATS, TILES * CHUNKS - (i * CHUNKS + chunk))
+            column = (i % TILES_IMAGE * CHUNKS + chunk) * WEIGHTS
+            repeats = REPEATS if i < TILES - SUM_LATE - 1 else REPEATS_LAST
+            bank = sums_ps[i // TILES_IMAGE][:].rearrange("p h t c w -> p (h t c w)")
             nc.tensor.matmul(
-                out=sums_ps[:, column : column + repeats * WEIGHTS],
+                out=bank[:, column : column + repeats * WEIGHTS],
                 lhsT=products_of[i][:, chunk * P : (chunk + 1) * P],
                 rhs=weights[:, i, :].unsqueeze(1).to_broadcast([P, repeats, WEIGHTS]),
                 start=True,
                 stop=True,
             )
 
-        for part in range(STEP):
-            regroup(0, part, nc.vector.tensor_copy)
-        quantise(0)
+        def add_tiles(b):
+            nc.vector.tensor_reduce(
+                out=result[:, 0:GROUPS].rearrange("p (w b c) -> p b c w", b=IMAGES, c=CHUNKS)[:, b, :, :],
+                in_=sums_ps[b][:, 0, :, :, :].rearrange("p t c w -> p c w t"),
+                axis=mybir.AxisListType.X,
+                op=ALU.add,
+            )
+
+        regroup(0, 0, nc.vector.tensor_copy)
+        regroup(0, 2, nc.scalar.copy)
+        regroup(0, 3, nc.scalar.copy)
+        quantise(0, 0, 1)
+        regroup(0, 1, nc.vector.tensor_copy)
+        quantise(0, 1, 1)
+        quantise(0, 2, 2)
         bias = keep.tile([P, 2 * CHANNELS], F32)
         for side in range(2):
             bias_ps = psum.tile([P, CHANNELS], F32, name="bank", tag="bank", bufs=BANKS)
             here = slice(CHANNELS * side, CHANNELS * (side + 1))
             nc.tensor.matmul(out=bias_ps[:], lhsT=ones[:], rhs=bias_row[:, here], start=True, stop=True)
             nc.scalar.copy(out=bias[:, here], in_=bias_ps[:])
+        mask_ps = psum.tile([P, P], BF16, name="bank", tag="bank", bufs=BANKS)
+        nc.tensor.transpose(mask_ps[:], mask_rows[:], ident_bf[:])
+        shares = keep.tile([P, TILES, WEIGHTS], F32)
+        nc.scalar.activation(
+            out=shares[:, :, 0], in_=mask_ps[:, 0:TILES], func=ACT.Copy, bias=1.0, scale=-1.0
+        )
+        nc.scalar.copy(out=shares[:, :, 1], in_=mask_ps[:, 0:TILES])
         for i in range(FEED_AHEAD):
             feed(i, 0)
             feed(i, 1)
-        mask_ps = psum.tile([P, P], BF16, name="bank", tag="bank", bufs=BANKS)
-        nc.tensor.transpose(mask_ps[:], mask_rows[:], ident_bf[:])
-        m_col = keep.tile([P, TILES], F32)
-        nc.scalar.copy(out=m_col[:], in_=mask_ps[:, 0:TILES])
-        for part in range(STEP):
-            regroup(1, part, nc.vector.tensor_copy)
-        quantise(1)
-        for part in range(STEP):
-            regroup(2, part, nc.scalar.copy)
+        regroup(1, 2, nc.scalar.copy)
+        regroup(1, 3, nc.scalar.copy)
 
         for i in range(TILES):
             s = i // STEP
@@ -215,10 +244,13 @@ def tile_hydraattention_pa_t_kernel(tc, x, mask, w_words, w_scales, b_kv, out_kn
                 invert_norm(i - 1)
             regroup(s + REGROUP_AHEAD, i % STEP, nc.scalar.copy)
             if i > 0:
-                weigh_mask(i - 1)
+                weigh(i - 1)
             feed(i + FEED_AHEAD, 0)
             for chunk in range(2):
                 sum_pixels(i - SUM_LATE, chunk)
+            if i == 0:
+                regroup(1, 0, nc.vector.tensor_copy)
+                regroup(1, 1, nc.vector.tensor_copy)
             values_of[i] = add_bias(i, 1)
             multiply(i)
             feed(i + FEED_AHEAD, 1)
@@ -226,27 +258,19 @@ def tile_hydraattention_pa_t_kernel(tc, x, mask, w_words, w_scales, b_kv, out_kn
                 sum_pixels(i - SUM_LATE, chunk)
             if i % STEP == 0:
                 quantise(s + QUANTISE_AHEAD)
+            if i == TILES_IMAGE + 2 * SUM_LATE + 2:
+                add_tiles(0)
         invert_norm(TILES - 1)
-        weigh_mask(TILES - 1)
+        weigh(TILES - 1)
         for i in range(TILES - SUM_LATE, TILES):
             for chunk in range(CHUNKS):
                 sum_pixels(i, chunk)
 
-        groups = IMAGES * CHUNKS
-        total = keep.tile([P, groups, WEIGHTS], F32)
-        width = TILES // IMAGES * CHUNKS * WEIGHTS
-        for b in range(IMAGES):
-            nc.vector.tensor_reduce(
-                out=total[:, b * CHUNKS : (b + 1) * CHUNKS, :],
-                in_=sums_ps[:, b * width : (b + 1) * width].rearrange("p (t c w) -> p c w t", c=CHUNKS, w=WEIGHTS),
-                axis=mybir.AxisListType.X,
-                op=ALU.add,
-            )
-        nc.vector.tensor_copy(out=result[:, groups : 2 * groups], in_=total[:, :, 1])
-        nc.vector.tensor_tensor(out=result[:, 0:groups], in0=total[:, :, 0], in1=total[:, :, 1], op=ALU.subtract)
+        add_tiles(1)
         rows_ps = psum.tile([P, P], F32, name="bank", tag="bank", bufs=BANKS)
         nc.tensor.transpose(rows_ps[:], result[:], ident_f32[:])
-        rows = keep.tile([2 * groups, P], F32)
-        nc.scalar.copy(out=rows[:], in_=rows_ps[0 : 2 * groups, :])
-        nc.sync.dma_start(out=out_know.rearrange("b o (j p) -> (b o j) p", p=P), in_=rows[0:groups, :])
-        nc.sync.dma_start(out=out_mask.rearrange("b o (j p) -> (b o j) p", p=P), in_=rows[groups : 2 * groups, :])
+        rows = keep.tile([GROUPS, P], F32)
+        nc.scalar.copy(out=rows[:], in_=rows_ps[0:GROUPS, :])
+        half = GROUPS // WEIGHTS
+        nc.sync.dma_start(out=out_know.rearrange("b o (j p) -> (b o j) p", p=P), in_=rows[0:half, :])
+        nc.scalar.dma_start(out=out_mask.rearrange("b o (j p) -> (b o j) p", p=P), in_=rows[half:GROUPS, :])

@@ -92,7 +92,12 @@ def tile_hydraattention_pa_t_kernel(tc, x, mask, w_words, w_scales, b_kv, out_kn
         square_sums = keep.tile([P, TILES], F32)
         inv_norm = keep.tile([P, TILES], F32)
         weights = keep.tile([P, TILES, WEIGHTS], F32)
-        sums_ps = [psum.tile([P, 2, TILES_IMAGE, CHUNKS, WEIGHTS], F32, name="sums%d" % b) for b in range(IMAGES)]
+        sums_ps = []
+
+        def open_sums(b):
+            sums_ps.append(psum.tile([P, 2, TILES_IMAGE, CHUNKS, WEIGHTS], F32, name="sums", tag="sums%d" % b))
+
+        open_sums(0)
 
         grouped_of = {}
         codes_of = {}
@@ -223,16 +228,17 @@ def tile_hydraattention_pa_t_kernel(tc, x, mask, w_words, w_scales, b_kv, out_kn
             here = slice(CHANNELS * side, CHANNELS * (side + 1))
             nc.tensor.matmul(out=bias_ps[:], lhsT=ones[:], rhs=bias_row[:, here], start=True, stop=True)
             nc.scalar.copy(out=bias[:, here], in_=bias_ps[:])
-        mask_ps = psum.tile([P, P], BF16, name="bank", tag="bank", bufs=BANKS)
+        for i in range(FEED_AHEAD):
+            feed(i, 0)
+            feed(i, 1)
+        mask_ps = psum.tile([P, P], BF16, name="mask_ps", tag="sums1")
         nc.tensor.transpose(mask_ps[:], mask_rows[:], ident_bf[:])
         shares = keep.tile([P, TILES, WEIGHTS], F32)
         nc.scalar.activation(
             out=shares[:, :, 0], in_=mask_ps[:, 0:TILES], func=ACT.Copy, bias=1.0, scale=-1.0
         )
         nc.scalar.copy(out=shares[:, :, 1], in_=mask_ps[:, 0:TILES])
-        for i in range(FEED_AHEAD):
-            feed(i, 0)
-            feed(i, 1)
+        open_sums(1)
         regroup(1, 2, nc.scalar.copy)
         regroup(1, 3, nc.scalar.copy)
 
@@ -245,16 +251,14 @@ def tile_hydraattention_pa_t_kernel(tc, x, mask, w_words, w_scales, b_kv, out_kn
             regroup(s + REGROUP_AHEAD, i % STEP, nc.scalar.copy)
             if i > 0:
                 weigh(i - 1)
-            feed(i + FEED_AHEAD, 0)
-            for chunk in range(2):
-                sum_pixels(i - SUM_LATE, chunk)
             if i == 0:
                 regroup(1, 0, nc.vector.tensor_copy)
                 regroup(1, 1, nc.vector.tensor_copy)
             values_of[i] = add_bias(i, 1)
             multiply(i)
+            feed(i + FEED_AHEAD, 0)
             feed(i + FEED_AHEAD, 1)
-            for chunk in range(2, CHUNKS):
+            for chunk in range(CHUNKS):
                 sum_pixels(i - SUM_LATE, chunk)
             if i % STEP == 0:
                 quantise(s + QUANTISE_AHEAD)

@@ -248,17 +248,22 @@ def tile_hydraattention_pa_t_kernel(tc, x, mask, w_words, w_scales, b_kv, out_kn
             square_key(i)
             if i > 0:
                 invert_norm(i - 1)
-            regroup(s + REGROUP_AHEAD, i % STEP, nc.scalar.copy)
+            if i % STEP < STEP - 1:
+                regroup(s + REGROUP_AHEAD, i % STEP, nc.scalar.copy)
+            else:
+                regroup(s + REGROUP_AHEAD, i % STEP, nc.vector.tensor_copy)
             if i > 0:
                 weigh(i - 1)
+            feed(i + FEED_AHEAD, 0)
+            for chunk in range(2):
+                sum_pixels(i - SUM_LATE, chunk)
             if i == 0:
                 regroup(1, 0, nc.vector.tensor_copy)
                 regroup(1, 1, nc.vector.tensor_copy)
             values_of[i] = add_bias(i, 1)
             multiply(i)
-            feed(i + FEED_AHEAD, 0)
             feed(i + FEED_AHEAD, 1)
-            for chunk in range(CHUNKS):
+            for chunk in range(2, CHUNKS):
                 sum_pixels(i - SUM_LATE, chunk)
             if i % STEP == 0:
                 quantise(s + QUANTISE_AHEAD)

@@ -33,6 +33,7 @@ BANKS = 6
 
 QUANTISE_AHEAD = 1
 REGROUP_AHEAD = 2
+VECTOR_TURN = 4
 FEED_AHEAD = 3
 SUM_LATE = 2
 REPEATS = 16
@@ -173,8 +174,10 @@ def tile_hydraattention_pa_t_kernel(tc, x, mask, w_words, w_scales, b_kv, out_kn
 
         def multiply(i):
             product = work.tile([P, CHANNELS], F32, name="product", tag="product", bufs=SUM_LATE + 3)
-            if i < TILES - 1:
+            if i < TILES - 1 and i % VECTOR_TURN < VECTOR_TURN - 1:
                 nc.gpsimd.tensor_tensor(out=product[:], in0=keys_of[i][:], in1=values_of[i][:], op=ALU.mult)
+            elif i < TILES - 1:
+                nc.vector.tensor_tensor(out=product[:], in0=keys_of[i][:], in1=values_of[i][:], op=ALU.mult)
             else:
                 for half in range(2):
                     here = slice(half * CHANNELS // 2, (half + 1) * CHANNELS // 2)
@@ -245,13 +248,12 @@ def tile_hydraattention_pa_t_kernel(tc, x, mask, w_words, w_scales, b_kv, out_kn
         for i in range(TILES):
             s = i // STEP
             keys_of[i] = add_bias(i, 0)
+            if i % VECTOR_TURN == 0 and i > 0:
+                multiply(i - 1)
             square_key(i)
             if i > 0:
                 invert_norm(i - 1)
-            if i % STEP < STEP - 1:
-                regroup(s + REGROUP_AHEAD, i % STEP, nc.scalar.copy)
-            else:
-                regroup(s + REGROUP_AHEAD, i % STEP, nc.vector.tensor_copy)
+            regroup(s + REGROUP_AHEAD, i % STEP, nc.scalar.copy)
             if i > 0:
                 weigh(i - 1)
             feed(i + FEED_AHEAD, 0)
@@ -261,7 +263,8 @@ def tile_hydraattention_pa_t_kernel(tc, x, mask, w_words, w_scales, b_kv, out_kn
                 regroup(1, 0, nc.vector.tensor_copy)
                 regroup(1, 1, nc.vector.tensor_copy)
             values_of[i] = add_bias(i, 1)
-            multiply(i)
+            if i % VECTOR_TURN < VECTOR_TURN - 1 or i == TILES - 1:
+                multiply(i)
             feed(i + FEED_AHEAD, 1)
             for chunk in range(2, CHUNKS):
                 sum_pixels(i - SUM_LATE, chunk)

@@ -27,7 +27,7 @@ STEPS_IMAGE = STEPS // IMAGES
 STEP_PIXELS = STEP * P
 WEIGHTS = 2
 
-GROUPS = WEIGHTS * IMAGES * CHUNKS
+GROUPS = WEIGHTS * CHUNKS
 
 BANKS = 6
 
@@ -37,7 +37,7 @@ VECTOR_TURN = 4
 FEED_AHEAD = 3
 SUM_LATE = 2
 REPEATS = 16
-REPEATS_LAST = 32
+SLOTS = 5
 
 
 def tile_hydraattention_pa_t_kernel(tc, x, mask, w_words, w_scales, b_kv, out_know, out_mask):
@@ -92,13 +92,13 @@ def tile_hydraattention_pa_t_kernel(tc, x, mask, w_words, w_scales, b_kv, out_kn
 
         square_sums = keep.tile([P, TILES], F32)
         inv_norm = keep.tile([P, TILES], F32)
-        weights = keep.tile([P, TILES, WEIGHTS], F32)
-        sums_ps = []
-
-        def open_sums(b):
-            sums_ps.append(psum.tile([P, 2, TILES_IMAGE, CHUNKS, WEIGHTS], F32, name="sums", tag="sums%d" % b))
-
-        open_sums(0)
+        weights = keep.tile([P, TILES_IMAGE, WEIGHTS], F32)
+        weight_slots = []
+        for slot in range(SLOTS):
+            weight_slot = keep.tile([P, P], F32, name="weight_slot%d" % slot)
+            nc.gpsimd.memset(weight_slot[:], 0.0)
+            weight_slots.append(weight_slot)
+        sums_ps = [psum.tile([P, 2, TILES_IMAGE, CHUNKS, WEIGHTS], F32, name="sums", tag="sums0")]
 
         grouped_of = {}
         codes_of = {}
@@ -192,31 +192,45 @@ def tile_hydraattention_pa_t_kernel(tc, x, mask, w_words, w_scales, b_kv, out_kn
             )
 
         def weigh(i):
-            nc.scalar.activation(
-                out=weights[:, i, :], in_=shares[:, i, :], func=ACT.Copy, scale=inv_norm[:, i : i + 1]
-            )
+            out = weights[:, i, :] if i < TILES_IMAGE else weight_slots[i % SLOTS][:, 0:WEIGHTS]
+            nc.scalar.activation(out=out, in_=shares[:, i, :], func=ACT.Copy, scale=inv_norm[:, i : i + 1])
 
-        def sum_pixels(i, chunk):
+        def sum_pixels(i, half):
             if i < 0:
                 return
-            column = (i % TILES_IMAGE * CHUNKS + chunk) * WEIGHTS
-            repeats = REPEATS if i < TILES - SUM_LATE - 1 else REPEATS_LAST
-            bank = sums_ps[i // TILES_IMAGE][:].rearrange("p h t c w -> p (h t c w)")
-            nc.tensor.matmul(
-                out=bank[:, column : column + repeats * WEIGHTS],
-                lhsT=products_of[i][:, chunk * P : (chunk + 1) * P],
-                rhs=weights[:, i, :].unsqueeze(1).to_broadcast([P, repeats, WEIGHTS]),
-                start=True,
-                stop=True,
-            )
+            if i < TILES_IMAGE:
+                bank = sums_ps[0][:].rearrange("p h t c w -> p (h t c w)")
+                for chunk in (2 * half, 2 * half + 1):
+                    column = (i * CHUNKS + chunk) * WEIGHTS
+                    nc.tensor.matmul(
+                        out=bank[:, column : column + REPEATS * WEIGHTS],
+                        lhsT=products_of[i][:, chunk * P : (chunk + 1) * P],
+                        rhs=weights[:, i, :].unsqueeze(1).to_broadcast([P, REPEATS, WEIGHTS]),
+                        start=True,
+                        stop=True,
+                    )
+            elif half == 1:
+                nc.tensor.matmul(
+                    out=sums_ps[1][:],
+                    lhsT=weight_slots[i % SLOTS][:],
+                    rhs=products_of[i][:],
+                    start=i == TILES_IMAGE,
+                    stop=i == TILES - 1,
+                )
 
-        def add_tiles(b):
+        def finish_first():
             nc.vector.tensor_reduce(
-                out=result[:, 0:GROUPS].rearrange("p (w b c) -> p b c w", b=IMAGES, c=CHUNKS)[:, b, :, :],
-                in_=sums_ps[b][:, 0, :, :, :].rearrange("p t c w -> p c w t"),
+                out=result[:, 0:GROUPS].rearrange("p (w c) -> p c w", c=CHUNKS),
+                in_=sums_ps[0][:, 0, :, :, :].rearrange("p t c w -> p c w t"),
                 axis=mybir.AxisListType.X,
                 op=ALU.add,
             )
+            rows_ps = psum.tile([P, P], F32, name="rows_ps", tag="sums0")
+            nc.tensor.transpose(rows_ps[:], result[:], ident_f32[:])
+            rows = keep.tile([GROUPS, P], F32)
+            nc.scalar.copy(out=rows[:], in_=rows_ps[0:GROUPS, :])
+            nc.sync.dma_start(out=out_know[0].rearrange("o (j p) -> (o j) p", p=P), in_=rows[0:CHUNKS, :])
+            nc.sync.dma_start(out=out_mask[0].rearrange("o (j p) -> (o j) p", p=P), in_=rows[CHUNKS:GROUPS, :])
 
         regroup(0, 0, nc.vector.tensor_copy)
         regroup(0, 2, nc.scalar.copy)
@@ -241,7 +255,7 @@ def tile_hydraattention_pa_t_kernel(tc, x, mask, w_words, w_scales, b_kv, out_kn
             out=shares[:, :, 0], in_=mask_ps[:, 0:TILES], func=ACT.Copy, bias=1.0, scale=-1.0
         )
         nc.scalar.copy(out=shares[:, :, 1], in_=mask_ps[:, 0:TILES])
-        open_sums(1)
+        sums_ps.append(psum.tile([P, CHANNELS], F32, name="sums1", tag="sums1"))
         regroup(1, 2, nc.scalar.copy)
         regroup(1, 3, nc.scalar.copy)
 
@@ -257,8 +271,7 @@ def tile_hydraattention_pa_t_kernel(tc, x, mask, w_words, w_scales, b_kv, out_kn
             if i > 0:
                 weigh(i - 1)
             feed(i + FEED_AHEAD, 0)
-            for chunk in range(2):
-                sum_pixels(i - SUM_LATE, chunk)
+            sum_pixels(i - SUM_LATE, 0)
             if i == 0:
                 regroup(1, 0, nc.vector.tensor_copy)
                 regroup(1, 1, nc.vector.tensor_copy)
@@ -266,23 +279,17 @@ def tile_hydraattention_pa_t_kernel(tc, x, mask, w_words, w_scales, b_kv, out_kn
             if i % VECTOR_TURN < VECTOR_TURN - 1 or i == TILES - 1:
                 multiply(i)
             feed(i + FEED_AHEAD, 1)
-            for chunk in range(2, CHUNKS):
-                sum_pixels(i - SUM_LATE, chunk)
+            sum_pixels(i - SUM_LATE, 1)
             if i % STEP == 0:
                 quantise(s + QUANTISE_AHEAD)
             if i == TILES_IMAGE + 2 * SUM_LATE + 2:
-                add_tiles(0)
+                finish_first()
         invert_norm(TILES - 1)
         weigh(TILES - 1)
         for i in range(TILES - SUM_LATE, TILES):
-            for chunk in range(CHUNKS):
-                sum_pixels(i, chunk)
+            sum_pixels(i, 1)
 
-        add_tiles(1)
-        rows_ps = psum.tile([P, P], F32, name="bank", tag="bank", bufs=BANKS)
-        nc.tensor.transpose(rows_ps[:], result[:], ident_f32[:])
-        rows = keep.tile([GROUPS, P], F32)
-        nc.scalar.copy(out=rows[:], in_=rows_ps[0:GROUPS, :])
-        half = GROUPS // WEIGHTS
-        nc.sync.dma_start(out=out_know.rearrange("b o (j p) -> (b o j) p", p=P), in_=rows[0:half, :])
-        nc.scalar.dma_start(out=out_mask.rearrange("b o (j p) -> (b o j) p", p=P), in_=rows[half:GROUPS, :])
+        rows1 = keep.tile([WEIGHTS, CHANNELS], F32)
+        nc.scalar.copy(out=rows1[:], in_=sums_ps[1][0:WEIGHTS, :])
+        nc.sync.dma_start(out=out_know[1], in_=rows1[0:1, :])
+        nc.scalar.dma_start(out=out_mask[1], in_=rows1[1:2, :])

@@ -34,9 +34,11 @@ BANKS = 6
 QUANTISE_AHEAD = 1
 REGROUP_AHEAD = 2
 VECTOR_TURN = 4
+HEAD = 3
 FEED_AHEAD = 3
-SUM_LATE = 2
-REPEATS = 16
+SUM_LATE = 1
+THIN = 16
+REPEATS = 4
 SLOTS = 5
 
 
@@ -92,13 +94,14 @@ def tile_hydraattention_pa_t_kernel(tc, x, mask, w_words, w_scales, b_kv, out_kn
 
         square_sums = keep.tile([P, TILES], F32)
         inv_norm = keep.tile([P, TILES], F32)
-        weights = keep.tile([P, TILES_IMAGE, WEIGHTS], F32)
+        weights = keep.tile([P, THIN, WEIGHTS], F32)
         weight_slots = []
         for slot in range(SLOTS):
             weight_slot = keep.tile([P, P], F32, name="weight_slot%d" % slot)
             nc.gpsimd.memset(weight_slot[:], 0.0)
             weight_slots.append(weight_slot)
-        sums_ps = [psum.tile([P, 2, TILES_IMAGE, CHUNKS, WEIGHTS], F32, name="sums", tag="sums0")]
+        thin_ps = psum.tile([P, 2, THIN, CHUNKS, WEIGHTS], F32, name="thin_ps", tag="sums0")
+        pooled_ps = {}
 
         grouped_of = {}
         codes_of = {}
@@ -173,8 +176,8 @@ def tile_hydraattention_pa_t_kernel(tc, x, mask, w_words, w_scales, b_kv, out_kn
             )
 
         def multiply(i):
-            product = work.tile([P, CHANNELS], F32, name="product", tag="product", bufs=SUM_LATE + 3)
-            if i < TILES - 1 and i % VECTOR_TURN < VECTOR_TURN - 1:
+            product = work.tile([P, CHANNELS], F32, name="product", tag="product", bufs=5)
+            if HEAD <= i < TILES - 1 and i % VECTOR_TURN < VECTOR_TURN - 1:
                 nc.gpsimd.tensor_tensor(out=product[:], in0=keys_of[i][:], in1=values_of[i][:], op=ALU.mult)
             elif i < TILES - 1:
                 nc.vector.tensor_tensor(out=product[:], in0=keys_of[i][:], in1=values_of[i][:], op=ALU.mult)
@@ -192,14 +195,14 @@ def tile_hydraattention_pa_t_kernel(tc, x, mask, w_words, w_scales, b_kv, out_kn
             )
 
         def weigh(i):
-            out = weights[:, i, :] if i < TILES_IMAGE else weight_slots[i % SLOTS][:, 0:WEIGHTS]
+            out = weights[:, i, :] if i < THIN else weight_slots[i % SLOTS][:, 0:WEIGHTS]
             nc.scalar.activation(out=out, in_=shares[:, i, :], func=ACT.Copy, scale=inv_norm[:, i : i + 1])
 
         def sum_pixels(i, half):
             if i < 0:
                 return
-            if i < TILES_IMAGE:
-                bank = sums_ps[0][:].rearrange("p h t c w -> p (h t c w)")
+            if i < THIN:
+                bank = thin_ps[:].rearrange("p h t c w -> p (h t c w)")
                 for chunk in (2 * half, 2 * half + 1):
                     column = (i * CHUNKS + chunk) * WEIGHTS
                     nc.tensor.matmul(
@@ -210,71 +213,102 @@ def tile_hydraattention_pa_t_kernel(tc, x, mask, w_words, w_scales, b_kv, out_kn
                         stop=True,
                     )
             elif half == 1:
+                b = i // TILES_IMAGE
+                if b not in pooled_ps:
+                    pooled_ps[b] = psum.tile([P, CHANNELS], F32, name="pooled_ps", tag="sums%d" % (1 - b))
                 nc.tensor.matmul(
-                    out=sums_ps[1][:],
+                    out=pooled_ps[b][:],
                     lhsT=weight_slots[i % SLOTS][:],
                     rhs=products_of[i][:],
-                    start=i == TILES_IMAGE,
-                    stop=i == TILES - 1,
+                    start=i == (THIN if b == 0 else TILES_IMAGE),
+                    stop=i == (b + 1) * TILES_IMAGE - 1,
                 )
 
-        def finish_first():
+        def turn_thin():
             nc.vector.tensor_reduce(
                 out=result[:, 0:GROUPS].rearrange("p (w c) -> p c w", c=CHUNKS),
-                in_=sums_ps[0][:, 0, :, :, :].rearrange("p t c w -> p c w t"),
+                in_=thin_ps[:, 0, :, :, :].rearrange("p t c w -> p c w t"),
                 axis=mybir.AxisListType.X,
                 op=ALU.add,
             )
             rows_ps = psum.tile([P, P], F32, name="rows_ps", tag="sums0")
             nc.tensor.transpose(rows_ps[:], result[:], ident_f32[:])
+            return rows_ps
+
+        def park_thin(rows_ps):
             rows = keep.tile([GROUPS, P], F32)
             nc.scalar.copy(out=rows[:], in_=rows_ps[0:GROUPS, :])
-            nc.sync.dma_start(out=out_know[0].rearrange("o (j p) -> (o j) p", p=P), in_=rows[0:CHUNKS, :])
-            nc.sync.dma_start(out=out_mask[0].rearrange("o (j p) -> (o j) p", p=P), in_=rows[CHUNKS:GROUPS, :])
+            thin_rows = keep.tile([WEIGHTS, CHANNELS], F32)
+            for w, out in enumerate((out_know, out_mask)):
+                nc.sync.dma_start(
+                    out=out[0].rearrange("o (j p) -> (o j) p", p=P), in_=rows[w * CHUNKS : (w + 1) * CHUNKS, :]
+                )
+                nc.sync.dma_start(out=thin_rows[w : w + 1, :], in_=out[0])
+            return thin_rows
+
+        def store(b, rows):
+            nc.sync.dma_start(out=out_know[b], in_=rows[0:1, :])
+            nc.scalar.dma_start(out=out_mask[b], in_=rows[1:2, :])
+
+        def finish_first(thin_rows):
+            first_rows = keep.tile([WEIGHTS, CHANNELS], F32)
+            nc.vector.tensor_tensor(
+                out=first_rows[:], in0=pooled_ps[0][0:WEIGHTS, :], in1=thin_rows[:], op=ALU.add
+            )
+            store(0, first_rows)
+
+        def copy_gpsimd(out, in_):
+            nc.gpsimd.tensor_scalar(out=out, in0=in_, scalar1=1.0, scalar2=0.0, op0=ALU.mult, op1=ALU.add)
 
         regroup(0, 0, nc.vector.tensor_copy)
-        regroup(0, 2, nc.scalar.copy)
-        regroup(0, 3, nc.scalar.copy)
         quantise(0, 0, 1)
-        regroup(0, 1, nc.vector.tensor_copy)
+        for part in range(1, STEP):
+            regroup(0, part, nc.vector.tensor_copy)
         quantise(0, 1, 1)
         quantise(0, 2, 2)
         bias = keep.tile([P, 2 * CHANNELS], F32)
-        for side in range(2):
+        for side, copy in enumerate((nc.vector.tensor_copy, nc.scalar.copy)):
             bias_ps = psum.tile([P, CHANNELS], F32, name="bank", tag="bank", bufs=BANKS)
             here = slice(CHANNELS * side, CHANNELS * (side + 1))
             nc.tensor.matmul(out=bias_ps[:], lhsT=ones[:], rhs=bias_row[:, here], start=True, stop=True)
-            nc.scalar.copy(out=bias[:, here], in_=bias_ps[:])
-        for i in range(FEED_AHEAD):
-            feed(i, 0)
-            feed(i, 1)
+            copy(out=bias[:, here], in_=bias_ps[:])
+        feed(0, 0)
+        feed(0, 1)
         mask_ps = psum.tile([P, P], BF16, name="mask_ps", tag="sums1")
         nc.tensor.transpose(mask_ps[:], mask_rows[:], ident_bf[:])
-        shares = keep.tile([P, TILES, WEIGHTS], F32)
-        nc.scalar.activation(
-            out=shares[:, :, 0], in_=mask_ps[:, 0:TILES], func=ACT.Copy, bias=1.0, scale=-1.0
-        )
-        nc.scalar.copy(out=shares[:, :, 1], in_=mask_ps[:, 0:TILES])
-        sums_ps.append(psum.tile([P, CHANNELS], F32, name="sums1", tag="sums1"))
+        for i in range(1, FEED_AHEAD):
+            feed(i, 0)
+            feed(i, 1)
         regroup(1, 2, nc.scalar.copy)
         regroup(1, 3, nc.scalar.copy)
+        regroup(1, 0, copy_gpsimd)
+        regroup(1, 1, copy_gpsimd)
+        shares = keep.tile([P, TILES, WEIGHTS], F32)
+
+        def share_pixels():
+            nc.scalar.activation(
+                out=shares[:, :, 0], in_=mask_ps[:, 0:TILES], func=ACT.Copy, bias=1.0, scale=-1.0
+            )
+            nc.scalar.copy(out=shares[:, :, 1], in_=mask_ps[:, 0:TILES])
 
         for i in range(TILES):
             s = i // STEP
             keys_of[i] = add_bias(i, 0)
             if i % VECTOR_TURN == 0 and i > 0:
                 multiply(i - 1)
-            square_key(i)
-            if i > 0:
+            if i > HEAD:
                 invert_norm(i - 1)
-            regroup(s + REGROUP_AHEAD, i % STEP, nc.scalar.copy)
-            if i > 0:
+            square_key(i)
+            if i > HEAD:
                 weigh(i - 1)
+            if i == 0:
+                share_pixels()
+            if i < HEAD:
+                invert_norm(i)
+                weigh(i)
+            regroup(s + REGROUP_AHEAD, i % STEP, nc.scalar.copy)
             feed(i + FEED_AHEAD, 0)
             sum_pixels(i - SUM_LATE, 0)
-            if i == 0:
-                regroup(1, 0, nc.vector.tensor_copy)
-                regroup(1, 1, nc.vector.tensor_copy)
             values_of[i] = add_bias(i, 1)
             if i % VECTOR_TURN < VECTOR_TURN - 1 or i == TILES - 1:
                 multiply(i)
@@ -282,14 +316,17 @@ def tile_hydraattention_pa_t_kernel(tc, x, mask, w_words, w_scales, b_kv, out_kn
             sum_pixels(i - SUM_LATE, 1)
             if i % STEP == 0:
                 quantise(s + QUANTISE_AHEAD)
-            if i == TILES_IMAGE + 2 * SUM_LATE + 2:
-                finish_first()
+            if i == THIN + 5:
+                rows_ps = turn_thin()
+            if i == THIN + 10:
+                thin_rows = park_thin(rows_ps)
+            if i == TILES_IMAGE + 6:
+                finish_first(thin_rows)
         invert_norm(TILES - 1)
         weigh(TILES - 1)
         for i in range(TILES - SUM_LATE, TILES):
             sum_pixels(i, 1)
 
-        rows1 = keep.tile([WEIGHTS, CHANNELS], F32)
-        nc.scalar.copy(out=rows1[:], in_=sums_ps[1][0:WEIGHTS, :])
-        nc.sync.dma_start(out=out_know[1], in_=rows1[0:1, :])
-        nc.scalar.dma_start(out=out_mask[1], in_=rows1[1:2, :])
+        last_rows = keep.tile([WEIGHTS, CHANNELS], F32)
+        nc.scalar.copy(out=last_rows[:], in_=pooled_ps[1][0:WEIGHTS, :])
+        store(1, last_rows)

@@ -36,8 +36,9 @@ REGROUP_AHEAD = 2
 VECTOR_TURN = 4
 HEAD = 3
 FEED_AHEAD = 3
-SUM_LATE = 1
-THIN = 16
+THIN = [i for i in range(TILES_IMAGE) if i % 3 > 0]
+WARM_UPS = 4
+MERGE_LATE = 8
 REPEATS = 4
 SLOTS = 5
 
@@ -59,11 +60,9 @@ def tile_hydraattention_pa_t_kernel(tc, x, mask, w_words, w_scales, b_kv, out_kn
                 queue.dma_start(out=raw[:, :, start:end], in_=x_rows[:, :, first + start : first + end])
 
         load_step(0, [(0, P)])
-        load_step(0, [(P, STEP_PIXELS)], nc.scalar)
-        table_warmer = keep.tile([P, 1], F32)
-        nc.vector.memset(table_warmer[:], 1.0)
-        nc.scalar.activation(out=table_warmer[:], in_=table_warmer[:], func=ACT.Abs_reciprocal_sqrt)
-
+        bias_row = keep.tile([P, 2 * CHANNELS], BF16)
+        nc.vector.memset(bias_row[:].bitcast(I32), 0)
+        nc.scalar.dma_start(out=bias_row[0:1, :], in_=b_kv.rearrange("(r c) -> r c", r=1))
         w_plane = keep.tile([P, 2 * CHANNELS], U8, align_bytes=64)
         nc.vector.memset(w_plane[:].bitcast(I32), 0)
         for quad in range(4):
@@ -73,13 +72,18 @@ def tile_hydraattention_pa_t_kernel(tc, x, mask, w_words, w_scales, b_kv, out_kn
             )
         w_codes = keep.tile([P, 2 * 2 * CHANNELS], U8, align_bytes=64)
         nc.sync.dma_start(out=w_codes[:].bitcast(I32), in_=w_words[0].bitcast(I32))
+        load_step(0, [(P, STEP_PIXELS)], nc.scalar)
+        table_warmer = keep.tile([P, 1], F32)
+        nc.vector.memset(table_warmer[:], 1.0)
+        nc.scalar.activation(out=table_warmer[:], in_=table_warmer[:], func=ACT.Abs_reciprocal_sqrt)
 
-        bias_row = keep.tile([P, 2 * CHANNELS], BF16)
-        nc.vector.memset(bias_row[:].bitcast(I32), 0)
-        nc.scalar.dma_start(out=bias_row[0:1, :], in_=b_kv.rearrange("(r c) -> r c", r=1))
+        ones = keep.tile([P, P], BF16)
+        nc.gpsimd.memset(ones[:], 1.0)
+        zeros = keep.tile([P, CHANNELS], BF16)
+        nc.gpsimd.memset(zeros[:].bitcast(I32), 0)
         mask_rows = keep.tile([P, P], BF16)
-        nc.vector.memset(mask_rows[:], 0.0)
-        nc.scalar.dma_start(out=mask_rows[0:TILES, :], in_=mask.rearrange("b o (t r) w -> (b o t) (r w)", r=2))
+        nc.gpsimd.memset(mask_rows[:].bitcast(I32), 0)
+        nc.gpsimd.dma_start(out=mask_rows[0:TILES, :], in_=mask.rearrange("b o (t r) w -> (b o t) (r w)", r=2))
         for s in range(1, STEPS):
             load_step(s, [(0, STEP_PIXELS)])
 
@@ -87,20 +91,18 @@ def tile_hydraattention_pa_t_kernel(tc, x, mask, w_words, w_scales, b_kv, out_kn
         make_identity(nc, ident_bf[:])
         ident_f32 = keep.tile([P, P], F32)
         make_identity(nc, ident_f32[:])
-        ones = keep.tile([P, P], BF16)
-        nc.vector.memset(ones[:], 1.0)
         result = keep.tile([P, P], F32)
         nc.gpsimd.memset(result[:], 0.0)
 
         square_sums = keep.tile([P, TILES], F32)
         inv_norm = keep.tile([P, TILES], F32)
-        weights = keep.tile([P, THIN, WEIGHTS], F32)
+        weights = keep.tile([P, TILES, WEIGHTS], F32)
         weight_slots = []
         for slot in range(SLOTS):
             weight_slot = keep.tile([P, P], F32, name="weight_slot%d" % slot)
             nc.gpsimd.memset(weight_slot[:], 0.0)
             weight_slots.append(weight_slot)
-        thin_ps = psum.tile([P, 2, THIN, CHUNKS, WEIGHTS], F32, name="thin_ps", tag="sums0")
+        thin_ps = psum.tile([P, CHANNELS], F32, name="thin_ps", tag="thin")
         pooled_ps = {}
 
         grouped_of = {}
@@ -177,7 +179,7 @@ def tile_hydraattention_pa_t_kernel(tc, x, mask, w_words, w_scales, b_kv, out_kn
 
         def multiply(i):
             product = work.tile([P, CHANNELS], F32, name="product", tag="product", bufs=5)
-            if HEAD <= i < TILES - 1 and i % VECTOR_TURN < VECTOR_TURN - 1:
+            if 0 < i < TILES - 1 and i % VECTOR_TURN < VECTOR_TURN - 1:
                 nc.gpsimd.tensor_tensor(out=product[:], in0=keys_of[i][:], in1=values_of[i][:], op=ALU.mult)
             elif i < TILES - 1:
                 nc.vector.tensor_tensor(out=product[:], in0=keys_of[i][:], in1=values_of[i][:], op=ALU.mult)
@@ -195,49 +197,49 @@ def tile_hydraattention_pa_t_kernel(tc, x, mask, w_words, w_scales, b_kv, out_kn
             )
 
         def weigh(i):
-            out = weights[:, i, :] if i < THIN else weight_slots[i % SLOTS][:, 0:WEIGHTS]
+            out = weights[:, i, :] if i in THIN else weight_slots[i % SLOTS][:, 0:WEIGHTS]
             nc.scalar.activation(out=out, in_=shares[:, i, :], func=ACT.Copy, scale=inv_norm[:, i : i + 1])
 
-        def sum_pixels(i, half):
+        def sum_pixels(i):
             if i < 0:
                 return
-            if i < THIN:
-                bank = thin_ps[:].rearrange("p h t c w -> p (h t c w)")
-                for chunk in (2 * half, 2 * half + 1):
-                    column = (i * CHUNKS + chunk) * WEIGHTS
+            b = i // TILES_IMAGE
+            if i in THIN:
+                for chunk in range(CHUNKS):
+                    column = (THIN.index(i) * CHUNKS + chunk) * WEIGHTS
                     nc.tensor.matmul(
-                        out=bank[:, column : column + REPEATS * WEIGHTS],
+                        out=thin_ps[:, column : column + REPEATS * WEIGHTS],
                         lhsT=products_of[i][:, chunk * P : (chunk + 1) * P],
                         rhs=weights[:, i, :].unsqueeze(1).to_broadcast([P, REPEATS, WEIGHTS]),
                         start=True,
                         stop=True,
                     )
-            elif half == 1:
-                b = i // TILES_IMAGE
-                if b not in pooled_ps:
-                    pooled_ps[b] = psum.tile([P, CHANNELS], F32, name="pooled_ps", tag="sums%d" % (1 - b))
-                nc.tensor.matmul(
-                    out=pooled_ps[b][:],
-                    lhsT=weight_slots[i % SLOTS][:],
-                    rhs=products_of[i][:],
-                    start=i == (THIN if b == 0 else TILES_IMAGE),
-                    stop=i == (b + 1) * TILES_IMAGE - 1,
-                )
+                return
+            first = b not in pooled_ps
+            if first:
+                pooled_ps[b] = psum.tile([P, CHANNELS], F32, name="pooled_ps", tag="pooled")
+            nc.tensor.matmul(
+                out=pooled_ps[b][:],
+                lhsT=weight_slots[i % SLOTS][:],
+                rhs=products_of[i][:],
+                start=first,
+                stop=i in (TILES_IMAGE - 2, TILES - 1),
+            )
 
         def turn_thin():
             nc.vector.tensor_reduce(
                 out=result[:, 0:GROUPS].rearrange("p (w c) -> p c w", c=CHUNKS),
-                in_=thin_ps[:, 0, :, :, :].rearrange("p t c w -> p c w t"),
+                in_=thin_ps[:, 0 : len(THIN) * CHUNKS * WEIGHTS].rearrange(
+                    "p (t c w) -> p c w t", c=CHUNKS, w=WEIGHTS
+                ),
                 axis=mybir.AxisListType.X,
                 op=ALU.add,
             )
-            rows_ps = psum.tile([P, P], F32, name="rows_ps", tag="sums0")
-            nc.tensor.transpose(rows_ps[:], result[:], ident_f32[:])
-            return rows_ps
+            nc.tensor.transpose(thin_ps[:, 2 * P : 3 * P], result[:], ident_f32[:])
 
-        def park_thin(rows_ps):
+        def park_thin():
             rows = keep.tile([GROUPS, P], F32)
-            nc.scalar.copy(out=rows[:], in_=rows_ps[0:GROUPS, :])
+            nc.scalar.copy(out=rows[:], in_=thin_ps[0:GROUPS, 2 * P : 3 * P])
             thin_rows = keep.tile([WEIGHTS, CHANNELS], F32)
             for w, out in enumerate((out_know, out_mask)):
                 nc.sync.dma_start(
@@ -250,16 +252,9 @@ def tile_hydraattention_pa_t_kernel(tc, x, mask, w_words, w_scales, b_kv, out_kn
             nc.sync.dma_start(out=out_know[b], in_=rows[0:1, :])
             nc.scalar.dma_start(out=out_mask[b], in_=rows[1:2, :])
 
-        def finish_first(thin_rows):
-            first_rows = keep.tile([WEIGHTS, CHANNELS], F32)
-            nc.vector.tensor_tensor(
-                out=first_rows[:], in0=pooled_ps[0][0:WEIGHTS, :], in1=thin_rows[:], op=ALU.add
-            )
-            store(0, first_rows)
-
-        def copy_gpsimd(out, in_):
-            nc.gpsimd.tensor_scalar(out=out, in0=in_, scalar1=1.0, scalar2=0.0, op0=ALU.mult, op1=ALU.add)
-
+        for warm_up in range(WARM_UPS):
+            unread_ps = psum.tile([P, CHANNELS], F32, name="unread_ps", tag="bank", bufs=BANKS)
+            nc.tensor.matmul(out=unread_ps[:], lhsT=ones[:], rhs=zeros[:], start=True, stop=True)
         regroup(0, 0, nc.vector.tensor_copy)
         quantise(0, 0, 1)
         for part in range(1, STEP):
@@ -267,22 +262,18 @@ def tile_hydraattention_pa_t_kernel(tc, x, mask, w_words, w_scales, b_kv, out_kn
         quantise(0, 1, 1)
         quantise(0, 2, 2)
         bias = keep.tile([P, 2 * CHANNELS], F32)
-        for side, copy in enumerate((nc.vector.tensor_copy, nc.scalar.copy)):
+        for side in range(2):
             bias_ps = psum.tile([P, CHANNELS], F32, name="bank", tag="bank", bufs=BANKS)
             here = slice(CHANNELS * side, CHANNELS * (side + 1))
             nc.tensor.matmul(out=bias_ps[:], lhsT=ones[:], rhs=bias_row[:, here], start=True, stop=True)
-            copy(out=bias[:, here], in_=bias_ps[:])
-        feed(0, 0)
-        feed(0, 1)
-        mask_ps = psum.tile([P, P], BF16, name="mask_ps", tag="sums1")
+            nc.scalar.copy(out=bias[:, here], in_=bias_ps[:])
+            feed(0, side)
+        feed(1, 0)
+        feed(1, 1)
+        mask_ps = psum.tile([P, P], BF16, name="mask_ps", tag="pooled")
         nc.tensor.transpose(mask_ps[:], mask_rows[:], ident_bf[:])
-        for i in range(1, FEED_AHEAD):
-            feed(i, 0)
-            feed(i, 1)
-        regroup(1, 2, nc.scalar.copy)
-        regroup(1, 3, nc.scalar.copy)
-        regroup(1, 0, copy_gpsimd)
-        regroup(1, 1, copy_gpsimd)
+        feed(2, 0)
+        feed(2, 1)
         shares = keep.tile([P, TILES, WEIGHTS], F32)
 
         def share_pixels():
@@ -306,26 +297,41 @@ def tile_hydraattention_pa_t_kernel(tc, x, mask, w_words, w_scales, b_kv, out_kn
             if i < HEAD:
                 invert_norm(i)
                 weigh(i)
+            if i == 0:
+                regroup(1, 0, nc.scalar.copy)
+                regroup(1, 1, nc.scalar.copy)
             regroup(s + REGROUP_AHEAD, i % STEP, nc.scalar.copy)
-            feed(i + FEED_AHEAD, 0)
-            sum_pixels(i - SUM_LATE, 0)
+            if i > 1:
+                feed(i + FEED_AHEAD, 0)
             values_of[i] = add_bias(i, 1)
             if i % VECTOR_TURN < VECTOR_TURN - 1 or i == TILES - 1:
                 multiply(i)
-            feed(i + FEED_AHEAD, 1)
-            sum_pixels(i - SUM_LATE, 1)
-            if i % STEP == 0:
+            if i == 0:
+                regroup(1, 2, nc.vector.tensor_copy)
+                regroup(1, 3, nc.vector.tensor_copy)
+            if i == 1:
+                sum_pixels(0)
+            if i % STEP == (1 if s == 0 else 0):
                 quantise(s + QUANTISE_AHEAD)
-            if i == THIN + 5:
-                rows_ps = turn_thin()
-            if i == THIN + 10:
-                thin_rows = park_thin(rows_ps)
-            if i == TILES_IMAGE + 6:
-                finish_first(thin_rows)
+            if i <= 1:
+                feed(i + FEED_AHEAD, 0)
+            feed(i + FEED_AHEAD, 1)
+            if i != 1:
+                sum_pixels(i - 1)
+            if i == max(THIN) + MERGE_LATE:
+                turn_thin()
+            if i == max(THIN) + 2 * MERGE_LATE:
+                thin_rows = park_thin()
+            if i == TILES_IMAGE:
+                pooled_rows = keep.tile([WEIGHTS, CHANNELS], F32)
+                nc.scalar.copy(out=pooled_rows[:], in_=pooled_ps[0][0:WEIGHTS, :])
+            if i == max(THIN) + 3 * MERGE_LATE:
+                first_rows = keep.tile([WEIGHTS, CHANNELS], F32)
+                nc.vector.tensor_tensor(out=first_rows[:], in0=pooled_rows[:], in1=thin_rows[:], op=ALU.add)
+                store(0, first_rows)
         invert_norm(TILES - 1)
         weigh(TILES - 1)
-        for i in range(TILES - SUM_LATE, TILES):
-            sum_pixels(i, 1)
+        sum_pixels(TILES - 1)
 
         last_rows = keep.tile([WEIGHTS, CHANNELS], F32)
         nc.scalar.copy(out=last_rows[:], in_=pooled_ps[1][0:WEIGHTS, :])

@@ -27,7 +27,7 @@ STEPS_IMAGE = STEPS // IMAGES
 STEP_PIXELS = STEP * P
 WEIGHTS = 2
 
-GROUPS = WEIGHTS * CHUNKS
+GROUPS = WEIGHTS * IMAGES * CHUNKS
 
 BANKS = 6
 
@@ -36,11 +36,11 @@ REGROUP_AHEAD = 2
 VECTOR_TURN = 4
 HEAD = 3
 FEED_AHEAD = 3
-THIN = [i for i in range(TILES_IMAGE) if i % 3 > 0]
+NEAR_TILES = 4
+FIRST_LATE = 9
 WARM_UPS = 4
-MERGE_LATE = 8
-REPEATS = 4
-SLOTS = 5
+REPEATS = 16
+REPEATS_LAST = 32
 
 
 def tile_hydraattention_pa_t_kernel(tc, x, mask, w_words, w_scales, b_kv, out_know, out_mask):
@@ -97,13 +97,7 @@ def tile_hydraattention_pa_t_kernel(tc, x, mask, w_words, w_scales, b_kv, out_kn
         square_sums = keep.tile([P, TILES], F32)
         inv_norm = keep.tile([P, TILES], F32)
         weights = keep.tile([P, TILES, WEIGHTS], F32)
-        weight_slots = []
-        for slot in range(SLOTS):
-            weight_slot = keep.tile([P, P], F32, name="weight_slot%d" % slot)
-            nc.gpsimd.memset(weight_slot[:], 0.0)
-            weight_slots.append(weight_slot)
-        thin_ps = psum.tile([P, CHANNELS], F32, name="thin_ps", tag="thin")
-        pooled_ps = {}
+        sums_ps = [psum.tile([P, 2, TILES_IMAGE, CHUNKS, WEIGHTS], F32, name="sums", tag="sums0")]
 
         grouped_of = {}
         codes_of = {}
@@ -121,8 +115,8 @@ def tile_hydraattention_pa_t_kernel(tc, x, mask, w_words, w_scales, b_kv, out_kn
                 )
             here = slice(part * P, (part + 1) * P)
             copy(
-                out=grouped_of[s][:, here, :].rearrange("p (c i) j -> p c j i", i=4),
-                in_=raw_tiles[s][:, :, here].rearrange("p j (c i) -> p c j i", i=4),
+                out=grouped_of[s][:, here, :],
+                in_=raw_tiles[s][:, :, here].rearrange("p j t -> p t j"),
             )
 
         def quantise(s, first=0, tiles=STEP):
@@ -197,60 +191,34 @@ def tile_hydraattention_pa_t_kernel(tc, x, mask, w_words, w_scales, b_kv, out_kn
             )
 
         def weigh(i):
-            out = weights[:, i, :] if i in THIN else weight_slots[i % SLOTS][:, 0:WEIGHTS]
-            nc.scalar.activation(out=out, in_=shares[:, i, :], func=ACT.Copy, scale=inv_norm[:, i : i + 1])
-
-        def sum_pixels(i):
-            if i < 0:
-                return
-            b = i // TILES_IMAGE
-            if i in THIN:
-                for chunk in range(CHUNKS):
-                    column = (THIN.index(i) * CHUNKS + chunk) * WEIGHTS
-                    nc.tensor.matmul(
-                        out=thin_ps[:, column : column + REPEATS * WEIGHTS],
-                        lhsT=products_of[i][:, chunk * P : (chunk + 1) * P],
-                        rhs=weights[:, i, :].unsqueeze(1).to_broadcast([P, REPEATS, WEIGHTS]),
-                        start=True,
-                        stop=True,
-                    )
-                return
-            first = b not in pooled_ps
-            if first:
-                pooled_ps[b] = psum.tile([P, CHANNELS], F32, name="pooled_ps", tag="pooled")
-            nc.tensor.matmul(
-                out=pooled_ps[b][:],
-                lhsT=weight_slots[i % SLOTS][:],
-                rhs=products_of[i][:],
-                start=first,
-                stop=i in (TILES_IMAGE - 2, TILES - 1),
+            nc.scalar.activation(
+                out=weights[:, i, :], in_=shares[:, i, :], func=ACT.Copy, scale=inv_norm[:, i : i + 1]
             )
 
-        def turn_thin():
+        def sum_pixels(i, chunks):
+            if i < 0:
+                return
+            if i == TILES_IMAGE and chunks[0] == 0:
+                sums_ps.append(psum.tile([P, 2, TILES_IMAGE, CHUNKS, WEIGHTS], F32, name="sums", tag="sums1"))
+            bank = sums_ps[i // TILES_IMAGE][:].rearrange("p h t c w -> p (h t c w)")
+            repeats = REPEATS if i < TILES - 3 else REPEATS_LAST
+            for chunk in chunks:
+                column = (i % TILES_IMAGE * CHUNKS + chunk) * WEIGHTS
+                nc.tensor.matmul(
+                    out=bank[:, column : column + repeats * WEIGHTS],
+                    lhsT=products_of[i][:, chunk * P : (chunk + 1) * P],
+                    rhs=weights[:, i, :].unsqueeze(1).to_broadcast([P, repeats, WEIGHTS]),
+                    start=True,
+                    stop=True,
+                )
+
+        def add_tiles(b):
             nc.vector.tensor_reduce(
-                out=result[:, 0:GROUPS].rearrange("p (w c) -> p c w", c=CHUNKS),
-                in_=thin_ps[:, 0 : len(THIN) * CHUNKS * WEIGHTS].rearrange(
-                    "p (t c w) -> p c w t", c=CHUNKS, w=WEIGHTS
-                ),
+                out=result[:, 0:GROUPS].rearrange("p (w b c) -> p b c w", b=IMAGES, c=CHUNKS)[:, b, :, :],
+                in_=sums_ps[b][:, 0, :, :, :].rearrange("p t c w -> p c w t"),
                 axis=mybir.AxisListType.X,
                 op=ALU.add,
             )
-            nc.tensor.transpose(thin_ps[:, 2 * P : 3 * P], result[:], ident_f32[:])
-
-        def park_thin():
-            rows = keep.tile([GROUPS, P], F32)
-            nc.scalar.copy(out=rows[:], in_=thin_ps[0:GROUPS, 2 * P : 3 * P])
-            thin_rows = keep.tile([WEIGHTS, CHANNELS], F32)
-            for w, out in enumerate((out_know, out_mask)):
-                nc.sync.dma_start(
-                    out=out[0].rearrange("o (j p) -> (o j) p", p=P), in_=rows[w * CHUNKS : (w + 1) * CHUNKS, :]
-                )
-                nc.sync.dma_start(out=thin_rows[w : w + 1, :], in_=out[0])
-            return thin_rows
-
-        def store(b, rows):
-            nc.sync.dma_start(out=out_know[b], in_=rows[0:1, :])
-            nc.scalar.dma_start(out=out_mask[b], in_=rows[1:2, :])
 
         for warm_up in range(WARM_UPS):
             unread_ps = psum.tile([P, CHANNELS], F32, name="unread_ps", tag="bank", bufs=BANKS)
@@ -270,7 +238,7 @@ def tile_hydraattention_pa_t_kernel(tc, x, mask, w_words, w_scales, b_kv, out_kn
             feed(0, side)
         feed(1, 0)
         feed(1, 1)
-        mask_ps = psum.tile([P, P], BF16, name="mask_ps", tag="pooled")
+        mask_ps = psum.tile([P, P], BF16, name="mask_ps", tag="sums1")
         nc.tensor.transpose(mask_ps[:], mask_rows[:], ident_bf[:])
         feed(2, 0)
         feed(2, 1)
@@ -285,6 +253,9 @@ def tile_hydraattention_pa_t_kernel(tc, x, mask, w_words, w_scales, b_kv, out_kn
         for i in range(TILES):
             s = i // STEP
             keys_of[i] = add_bias(i, 0)
+            late = i - 1 if i <= NEAR_TILES else i - 2
+            if i == NEAR_TILES + 1:
+                late = None
             if i % VECTOR_TURN == 0 and i > 0:
                 multiply(i - 1)
             if i > HEAD:
@@ -303,6 +274,8 @@ def tile_hydraattention_pa_t_kernel(tc, x, mask, w_words, w_scales, b_kv, out_kn
             regroup(s + REGROUP_AHEAD, i % STEP, nc.scalar.copy)
             if i > 1:
                 feed(i + FEED_AHEAD, 0)
+                if late is not None:
+                    sum_pixels(late, range(2))
             values_of[i] = add_bias(i, 1)
             if i % VECTOR_TURN < VECTOR_TURN - 1 or i == TILES - 1:
                 multiply(i)
@@ -310,29 +283,26 @@ def tile_hydraattention_pa_t_kernel(tc, x, mask, w_words, w_scales, b_kv, out_kn
                 regroup(1, 2, nc.vector.tensor_copy)
                 regroup(1, 3, nc.vector.tensor_copy)
             if i == 1:
-                sum_pixels(0)
+                sum_pixels(0, range(CHUNKS))
             if i % STEP == (1 if s == 0 else 0):
                 quantise(s + QUANTISE_AHEAD)
             if i <= 1:
                 feed(i + FEED_AHEAD, 0)
             feed(i + FEED_AHEAD, 1)
-            if i != 1:
-                sum_pixels(i - 1)
-            if i == max(THIN) + MERGE_LATE:
-                turn_thin()
-            if i == max(THIN) + 2 * MERGE_LATE:
-                thin_rows = park_thin()
-            if i == TILES_IMAGE:
-                pooled_rows = keep.tile([WEIGHTS, CHANNELS], F32)
-                nc.scalar.copy(out=pooled_rows[:], in_=pooled_ps[0][0:WEIGHTS, :])
-            if i == max(THIN) + 3 * MERGE_LATE:
-                first_rows = keep.tile([WEIGHTS, CHANNELS], F32)
-                nc.vector.tensor_tensor(out=first_rows[:], in0=pooled_rows[:], in1=thin_rows[:], op=ALU.add)
-                store(0, first_rows)
+            if i > 1 and late is not None:
+                sum_pixels(late, range(2, CHUNKS))
+            if i == TILES_IMAGE - 1 + FIRST_LATE:
+                add_tiles(0)
         invert_norm(TILES - 1)
         weigh(TILES - 1)
-        sum_pixels(TILES - 1)
+        for i in (TILES - 2, TILES - 1):
+            sum_pixels(i, range(CHUNKS))
 
-        last_rows = keep.tile([WEIGHTS, CHANNELS], F32)
-        nc.scalar.copy(out=last_rows[:], in_=pooled_ps[1][0:WEIGHTS, :])
-        store(1, last_rows)
+        add_tiles(1)
+        rows_ps = psum.tile([P, P], F32, name="bank", tag="bank", bufs=BANKS)
+        nc.tensor.transpose(rows_ps[:], result[:], ident_f32[:])
+        rows = keep.tile([GROUPS, P], F32)
+        nc.scalar.copy(out=rows[:], in_=rows_ps[0:GROUPS, :])
+        half = GROUPS // WEIGHTS
+        nc.sync.dma_start(out=out_know.rearrange("b o (j p) -> (b o j) p", p=P), in_=rows[0:half, :])
+        nc.scalar.dma_start(out=out_mask.rearrange("b o (j p) -> (b o j) p", p=P), in_=rows[half:GROUPS, :])

@@ -173,7 +173,7 @@ def tile_hydraattention_pa_t_kernel(tc, x, mask, w_words, w_scales, b_kv, out_kn
 
         def multiply(i):
             product = work.tile([P, CHANNELS], F32, name="product", tag="product", bufs=5)
-            if 0 < i < TILES - 1 and i % VECTOR_TURN < VECTOR_TURN - 1:
+            if HEAD <= i < TILES - 1 and i % VECTOR_TURN < VECTOR_TURN - 1:
                 nc.gpsimd.tensor_tensor(out=product[:], in0=keys_of[i][:], in1=values_of[i][:], op=ALU.mult)
             elif i < TILES - 1:
                 nc.vector.tensor_tensor(out=product[:], in0=keys_of[i][:], in1=values_of[i][:], op=ALU.mult)
@@ -235,13 +235,19 @@ def tile_hydraattention_pa_t_kernel(tc, x, mask, w_words, w_scales, b_kv, out_kn
             here = slice(CHANNELS * side, CHANNELS * (side + 1))
             nc.tensor.matmul(out=bias_ps[:], lhsT=ones[:], rhs=bias_row[:, here], start=True, stop=True)
             nc.scalar.copy(out=bias[:, here], in_=bias_ps[:])
-            feed(0, side)
+        feed(0, 0)
+        feed(0, 1)
         feed(1, 0)
         feed(1, 1)
         mask_ps = psum.tile([P, P], BF16, name="mask_ps", tag="sums1")
         nc.tensor.transpose(mask_ps[:], mask_rows[:], ident_bf[:])
         feed(2, 0)
         feed(2, 1)
+        def copy_gpsimd(out, in_):
+            nc.gpsimd.tensor_scalar(out=out, in0=in_, scalar1=1.0, scalar2=0.0, op0=ALU.mult, op1=ALU.add)
+
+        regroup(1, 2, copy_gpsimd)
+        regroup(1, 3, copy_gpsimd)
         shares = keep.tile([P, TILES, WEIGHTS], F32)
 
         def share_pixels():
@@ -279,9 +285,6 @@ def tile_hydraattention_pa_t_kernel(tc, x, mask, w_words, w_scales, b_kv, out_kn
             values_of[i] = add_bias(i, 1)
             if i % VECTOR_TURN < VECTOR_TURN - 1 or i == TILES - 1:
                 multiply(i)
-            if i == 0:
-                regroup(1, 2, nc.vector.tensor_copy)
-                regroup(1, 3, nc.vector.tensor_copy)
             if i == 1:
                 sum_pixels(0, range(CHUNKS))
             if i % STEP == (1 if s == 0 else 0):

import concourse.mybir as mybir
from concourse.masks import make_identity

FLOPS = 2 * 2 * 4096 * 512 * 1024

F32 = mybir.dt.float32
BF16 = mybir.dt.bfloat16
U8 = mybir.dt.uint8
U32 = mybir.dt.uint32
I32 = mybir.dt.int32
FP8X4 = mybir.dt.float8_e4m3fn_x4
FP4X4 = mybir.dt.float4_e2m1fn_x4
ALU = mybir.AluOpType
ACT = mybir.ActivationFunctionType

P = 128
PACK = 4
IMAGES = 2
PIXELS = 4096
CHANNELS = 512
CHUNKS = CHANNELS // P
TILES = IMAGES * PIXELS // P
TILES_IMAGE = TILES // IMAGES
STEP = 4
STEPS = TILES // STEP
STEPS_IMAGE = STEPS // IMAGES
STEP_PIXELS = STEP * P
WEIGHTS = 2

GROUPS = WEIGHTS * IMAGES * CHUNKS

BANKS = 6

QUANTISE_AHEAD = 1
REGROUP_AHEAD = 2
VECTOR_TURN = 4
HEAD = 3
FEED_AHEAD = 3
NEAR_TILES = 4
FIRST_LATE = 9
WARM_UPS = 4
REPEATS = 16
REPEATS_LAST = 32


def tile_hydraattention_pa_t_kernel(tc, x, mask, w_words, w_scales, b_kv, out_know, out_mask):
    nc = tc.nc
    with tc.tile_pool(name="keep", bufs=1) as keep, tc.tile_pool(name="work", bufs=2) as work, tc.psum_pool(
        name="psum", bufs=1
    ) as psum, tc.manual_schedule():
        raw_tiles = []

        def load_step(s, pieces, queue=nc.sync):
            x_rows = x[s // STEPS_IMAGE].rearrange("(p j) h w -> p j (h w)", j=PACK)
            if s == len(raw_tiles):
                raw_tiles.append(keep.tile([P, PACK, STEP_PIXELS], BF16, name="raw%d" % s))
            raw = raw_tiles[s]
            first = s % STEPS_IMAGE * STEP_PIXELS
            for start, end in pieces:
                queue.dma_start(out=raw[:, :, start:end], in_=x_rows[:, :, first + start : first + end])

        load_step(0, [(0, P)])
        bias_row = keep.tile([P, 2 * CHANNELS], BF16)
        nc.vector.memset(bias_row[:].bitcast(I32), 0)
        nc.scalar.dma_start(out=bias_row[0:1, :], in_=b_kv.rearrange("(r c) -> r c", r=1))
        w_plane = keep.tile([P, 2 * CHANNELS], U8, align_bytes=64)
        nc.vector.memset(w_plane[:].bitcast(I32), 0)
        for quad in range(4):
            nc.sync.dma_start(
                out=w_plane[32 * quad : 32 * quad + 4, :].bitcast(I32),
                in_=w_scales[0, 4 * quad : 4 * quad + 4, :].bitcast(I32),
            )
        w_codes = keep.tile([P, 2 * 2 * CHANNELS], U8, align_bytes=64)
        nc.sync.dma_start(out=w_codes[:].bitcast(I32), in_=w_words[0].bitcast(I32))
        load_step(0, [(P, STEP_PIXELS)], nc.scalar)
        table_warmer = keep.tile([P, 1], F32)
        nc.vector.memset(table_warmer[:], 1.0)
        nc.scalar.activation(out=table_warmer[:], in_=table_warmer[:], func=ACT.Abs_reciprocal_sqrt)

        ones = keep.tile([P, P], BF16)
        nc.gpsimd.memset(ones[:], 1.0)
        zeros = keep.tile([P, CHANNELS], BF16)
        nc.gpsimd.memset(zeros[:].bitcast(I32), 0)
        mask_rows = keep.tile([P, P], BF16)
        nc.gpsimd.memset(mask_rows[:].bitcast(I32), 0)
        nc.gpsimd.dma_start(out=mask_rows[0:TILES, :], in_=mask.rearrange("b o (t r) w -> (b o t) (r w)", r=2))
        for s in range(1, STEPS):
            load_step(s, [(0, STEP_PIXELS)])

        ident_bf = keep.tile([P, P], BF16)
        make_identity(nc, ident_bf[:])
        ident_f32 = keep.tile([P, P], F32)
        make_identity(nc, ident_f32[:])
        result = keep.tile([P, P], F32)
        nc.gpsimd.memset(result[:], 0.0)

        square_sums = keep.tile([P, TILES], F32)
        inv_norm = keep.tile([P, TILES], F32)
        weights = keep.tile([P, TILES, WEIGHTS], F32)
        sums_ps = [psum.tile([P, 2, TILES_IMAGE, CHUNKS, WEIGHTS], F32, name="sums", tag="sums0")]

        grouped_of = {}
        codes_of = {}
        banks = {}
        keys_of = {}
        values_of = {}
        products_of = {}

        def regroup(s, part, copy):
            if s >= STEPS:
                return
            if s not in grouped_of:
                grouped_of[s] = work.tile(
                    [P, STEP_PIXELS, PACK], BF16, name="grouped", tag="grouped", bufs=3, align_bytes=64
                )
            here = slice(part * P, (part + 1) * P)
            copy(
                out=grouped_of[s][:, here, :],
                in_=raw_tiles[s][:, :, here].rearrange("p j t -> p t j"),
            )

        def quantise(s, first=0, tiles=STEP):
            if s >= STEPS:
                return
            if first == 0:
                x_codes = work.tile(
                    [P, STEP_PIXELS], U32, name="x_codes", tag="x_codes", bufs=QUANTISE_AHEAD + 2, align_bytes=64
                )
                x_plane = work.tile(
                    [P, STEP_PIXELS], U8, name="x_plane", tag="x_plane", bufs=QUANTISE_AHEAD + 2, align_bytes=64
                )
                codes_of[s] = (x_codes, x_plane)
            x_codes, x_plane = codes_of[s]
            here = slice(first * P, (first + tiles) * P)
            nc.vector.quantize_mx(
                out=x_codes[:, here].bitcast(FP8X4),
                scales=x_plane[:, here],
                in_=grouped_of[s][:, here, :].rearrange("p t j -> p (t j)"),
            )

        def feed(i, side):
            if i >= TILES:
                return
            x_codes, x_plane = codes_of[i // STEP]
            here = slice(i % STEP * P, (i % STEP + 1) * P)
            bank = psum.tile([P, CHANNELS], F32, name="bank", tag="bank", bufs=BANKS)
            nc.tensor.matmul_mx(
                out=bank[:],
                lhsT=x_codes[:, here].bitcast(FP8X4),
                lhsT_scale=x_plane[:, here],
                rhs=w_codes[:, 2 * CHANNELS * side : 2 * CHANNELS * (side + 1)].bitcast(FP4X4),
                rhs_scale=w_plane[:, CHANNELS * side : CHANNELS * (side + 1)],
                start=True,
                stop=True,
            )
            banks[(i, side)] = bank

        def add_bias(i, side):
            out = work.tile([P, CHANNELS], F32, name="keyval", tag="key" if side == 0 else "value", bufs=4)
            nc.vector.tensor_tensor(
                out=out[:],
                in0=banks[(i, side)][:],
                in1=bias[:, CHANNELS * side : CHANNELS * (side + 1)],
                op=ALU.add,
            )
            return out

        def square_key(i):
            unread = work.tile([P, CHANNELS], BF16, name="unread", tag="unread", bufs=2)
            nc.scalar.activation(
                out=unread[:], in_=keys_of[i][:], func=ACT.Square, accum_out=square_sums[:, i : i + 1]
            )

        def multiply(i):
            product = work.tile([P, CHANNELS], F32, name="product", tag="product", bufs=5)
            if HEAD <= i < TILES - 1 and i % VECTOR_TURN < VECTOR_TURN - 1:
                nc.gpsimd.tensor_tensor(out=product[:], in0=keys_of[i][:], in1=values_of[i][:], op=ALU.mult)
            elif i < TILES - 1:
                nc.vector.tensor_tensor(out=product[:], in0=keys_of[i][:], in1=values_of[i][:], op=ALU.mult)
            else:
                for half in range(2):
                    here = slice(half * CHANNELS // 2, (half + 1) * CHANNELS // 2)
                    nc.vector.tensor_tensor(
                        out=product[:, here], in0=keys_of[i][:, here], in1=values_of[i][:, here], op=ALU.mult
                    )
            products_of[i] = product

        def invert_norm(i):
            nc.scalar.activation(
                out=inv_norm[:, i : i + 1], in_=square_sums[:, i : i + 1], func=ACT.Abs_reciprocal_sqrt
            )

        def weigh(i):
            nc.scalar.activation(
                out=weights[:, i, :], in_=shares[:, i, :], func=ACT.Copy, scale=inv_norm[:, i : i + 1]
            )

        def sum_pixels(i, chunks):
            if i < 0:
                return
            if i == TILES_IMAGE and chunks[0] == 0:
                sums_ps.append(psum.tile([P, 2, TILES_IMAGE, CHUNKS, WEIGHTS], F32, name="sums", tag="sums1"))
            bank = sums_ps[i // TILES_IMAGE][:].rearrange("p h t c w -> p (h t c w)")
            repeats = REPEATS if i < TILES - 3 else REPEATS_LAST
            for chunk in chunks:
                column = (i % TILES_IMAGE * CHUNKS + chunk) * WEIGHTS
                nc.tensor.matmul(
                    out=bank[:, column : column + repeats * WEIGHTS],
                    lhsT=products_of[i][:, chunk * P : (chunk + 1) * P],
                    rhs=weights[:, i, :].unsqueeze(1).to_broadcast([P, repeats, WEIGHTS]),
                    start=True,
                    stop=True,
                )

        def add_tiles(b):
            nc.vector.tensor_reduce(
                out=result[:, 0:GROUPS].rearrange("p (w b c) -> p b c w", b=IMAGES, c=CHUNKS)[:, b, :, :],
                in_=sums_ps[b][:, 0, :, :, :].rearrange("p t c w -> p c w t"),
                axis=mybir.AxisListType.X,
                op=ALU.add,
            )

        for warm_up in range(WARM_UPS):
            unread_ps = psum.tile([P, CHANNELS], F32, name="unread_ps", tag="bank", bufs=BANKS)
            nc.tensor.matmul(out=unread_ps[:], lhsT=ones[:], rhs=zeros[:], start=True, stop=True)
        regroup(0, 0, nc.vector.tensor_copy)
        quantise(0, 0, 1)
        for part in range(1, STEP):
            regroup(0, part, nc.vector.tensor_copy)
        quantise(0, 1, 1)
        quantise(0, 2, 2)
        bias = keep.tile([P, 2 * CHANNELS], F32)
        for side in range(2):
            bias_ps = psum.tile([P, CHANNELS], F32, name="bank", tag="bank", bufs=BANKS)
            here = slice(CHANNELS * side, CHANNELS * (side + 1))
            nc.tensor.matmul(out=bias_ps[:], lhsT=ones[:], rhs=bias_row[:, here], start=True, stop=True)
            nc.scalar.copy(out=bias[:, here], in_=bias_ps[:])
        feed(0, 0)
        feed(0, 1)
        feed(1, 0)
        feed(1, 1)
        mask_ps = psum.tile([P, P], BF16, name="mask_ps", tag="sums1")
        nc.tensor.transpose(mask_ps[:], mask_rows[:], ident_bf[:])
        feed(2, 0)
        feed(2, 1)
        def copy_gpsimd(out, in_):
            nc.gpsimd.tensor_scalar(out=out, in0=in_, scalar1=1.0, scalar2=0.0, op0=ALU.mult, op1=ALU.add)

        regroup(1, 2, copy_gpsimd)
        regroup(1, 3, copy_gpsimd)
        shares = keep.tile([P, TILES, WEIGHTS], F32)

        def share_pixels():
            nc.scalar.activation(
                out=shares[:, :, 0], in_=mask_ps[:, 0:TILES], func=ACT.Copy, bias=1.0, scale=-1.0
            )
            nc.scalar.copy(out=shares[:, :, 1], in_=mask_ps[:, 0:TILES])

        for i in range(TILES):
            s = i // STEP
            keys_of[i] = add_bias(i, 0)
            late = i - 1 if i <= NEAR_TILES else i - 2
            if i == NEAR_TILES + 1:
                late = None
            if i % VECTOR_TURN == 0 and i > 0:
                multiply(i - 1)
            if i > HEAD:
                invert_norm(i - 1)
            square_key(i)
            if i > HEAD:
                weigh(i - 1)
            if i == 0:
                share_pixels()
            if i < HEAD:
                invert_norm(i)
                weigh(i)
            if i == 0:
                regroup(1, 0, nc.scalar.copy)
                regroup(1, 1, nc.scalar.copy)
            regroup(s + REGROUP_AHEAD, i % STEP, nc.scalar.copy)
            if i > 1:
                feed(i + FEED_AHEAD, 0)
                if late is not None:
                    sum_pixels(late, range(2))
            values_of[i] = add_bias(i, 1)
            if i % VECTOR_TURN < VECTOR_TURN - 1 or i == TILES - 1:
                multiply(i)
            if i == 1:
                sum_pixels(0, range(CHUNKS))
            if i % STEP == (1 if s == 0 else 0):
                quantise(s + QUANTISE_AHEAD)
            if i <= 1:
                feed(i + FEED_AHEAD, 0)
            feed(i + FEED_AHEAD, 1)
            if i > 1 and late is not None:
                sum_pixels(late, range(2, CHUNKS))
            if i == TILES_IMAGE - 1 + FIRST_LATE:
                add_tiles(0)
        invert_norm(TILES - 1)
        weigh(TILES - 1)
        for i in (TILES - 2, TILES - 1):
            sum_pixels(i, range(CHUNKS))

        add_tiles(1)
        rows_ps = psum.tile([P, P], F32, name="bank", tag="bank", bufs=BANKS)
        nc.tensor.transpose(rows_ps[:], result[:], ident_f32[:])
        rows = keep.tile([GROUPS, P], F32)
        nc.scalar.copy(out=rows[:], in_=rows_ps[0:GROUPS, :])
        half = GROUPS // WEIGHTS
        nc.sync.dma_start(out=out_know.rearrange("b o (j p) -> (b o j) p", p=P), in_=rows[0:half, :])
        nc.scalar.dma_start(out=out_mask.rearrange("b o (j p) -> (b o j) p", p=P), in_=rows[half:GROUPS, :])
